import numpy as np
import ml_dtypes


def mxq(x, axis, fmt="e4m3"):
    dtype, down = {"e4m3": (ml_dtypes.float8_e4m3fn, 7), "e5m2": (ml_dtypes.float8_e5m2, 14)}[fmt]
    v = np.moveaxis(np.asarray(x, np.float32).astype(ml_dtypes.bfloat16).astype(np.float64), axis, -1)
    blocks = v.reshape(v.shape[:-1] + (-1, 32))
    amax = np.abs(blocks).max(-1, keepdims=True)
    byte = np.maximum(np.where(amax > 0, np.frexp(amax)[1] - 1 + 127, 0) - down, 1)
    scale = np.exp2(byte - 127.0)
    codes = (blocks / scale).astype(np.float32).astype(dtype).astype(np.float64)
    return np.moveaxis((codes * scale).reshape(v.shape), -1, axis)


WIDE = False


def mx_kscale(k):
    if not WIDE:
        return np.ones(k)
    levels = np.array([10, -10, 5, -5, 0])
    a = np.random.permutation(np.resize(levels, k // 512 * 4)).reshape(k // 512, 4)
    idx = np.arange(k)
    return np.exp2(a[idx // 512, idx % 128 // 32])


BF16 = ml_dtypes.bfloat16


def bf(x):
    return np.asarray(x, np.float32).astype(BF16)


def f64(x):
    return np.asarray(x).astype(np.float64)


E2M1 = np.array([0.0, 0.5, 1.0, 1.5, 2.0, 3.0, 4.0, 6.0, -0.0, -0.5, -1.0, -1.5, -2.0, -3.0, -4.0, -6.0])


def pack_weight(w, fmt):
    k, n = w.shape
    w = f64(bf(w)).reshape(k // 32, 32, n)
    amax = np.abs(w).max(1)
    if fmt == "e4m3":
        byte = np.frexp(amax)[1] - 1 + 127 - 7
    else:
        mant, ex = np.frexp(amax / 6.0)
        byte = np.where(mant > 0.5, ex, ex - 1) + 127
    byte = np.clip(np.where(amax > 0, byte, 1), 1, 254)
    scaled = (w * np.exp2(127.0 - byte)[:, None, :]).reshape(k, n).astype(np.float32)
    by_word = np.ascontiguousarray(scaled.reshape(k // 512, 128, 4, n).transpose(0, 1, 3, 2))
    if fmt == "e4m3":
        words = by_word.astype(ml_dtypes.float8_e4m3fn).view(np.uint8)
    else:
        c = by_word.astype(ml_dtypes.float4_e2m1fn).view(np.uint8) & 0xF
        words = c[..., 0::2] | (c[..., 1::2] << 4)
    return np.ascontiguousarray(words), np.ascontiguousarray(byte.astype(np.uint8).reshape(k // 512, 16, n))


def unpack_weight(words, scales, fmt):
    g, p, n, _ = words.shape
    if fmt == "e4m3":
        vals = np.ascontiguousarray(words).view(ml_dtypes.float8_e4m3fn).astype(np.float64)
    else:
        nib = np.empty((g, p, n, 4), np.uint8)
        nib[..., 0::2] = words & 0xF
        nib[..., 1::2] = words >> 4
        vals = E2M1[nib]
    vals = vals * np.repeat(np.exp2(scales.astype(np.float64) - 127.0), 8, axis=1)[..., None]
    return vals.transpose(0, 1, 3, 2).reshape(g * 512, n)


B, LQ, LK, DIN, H = 2, 2048, 1024, 1024, 512
FLOOR = 1e-9
FMT = "e4m3"


def setup_inputs():
    s = mx_kscale(DIN)
    mass = np.where(np.random.random((B, LQ, 1)) < 0.25, FLOOR, 1.0)
    q = bf(np.random.standard_normal((B, LQ, H)) * 1.5)
    k = bf(np.random.standard_normal((B, LK, H)) * 1.5)
    v_ret = bf(np.random.standard_normal((B, LK, DIN)) * s)
    pi_star = bf(mass * np.exp(1.25 * np.random.standard_normal((B, LQ, LK))))
    Wv_words, Wv_scales = pack_weight(np.random.standard_normal((DIN, H)) * 1.5 / np.sqrt(DIN) / s[:, None], FMT)
    bv = bf(np.random.standard_normal(H) * 0.25)
    gamma = bf(1.25 + 0.25 * np.random.random(1))
    return {"q": q,
            "k": k,
            "v_ret": v_ret,
            "pi_star": pi_star,
            "Wv_words": Wv_words,
            "Wv_scales": Wv_scales,
            "bv": bv,
            "gamma": gamma}


def reference(q, k, v_ret, pi_star, Wv_words, Wv_scales, bv, gamma):
    wvq = unpack_weight(Wv_words, Wv_scales, FMT)
    rows = []
    for b in range(B):
        v = (mxq(f64(v_ret[b]), 1, "e4m3") @ wvq) + f64(bv)
        logits = f64(q[b]) @ f64(k[b]).T / np.sqrt(H)
        z = logits + f64(gamma) * np.log(np.maximum(f64(pi_star[b]), FLOOR))
        e = np.exp(z - z.max(1, keepdims=True))
        rows.append((mxq(e, 1, "e4m3") @ mxq(v, 0, "e4m3")) / e.sum(1, keepdims=True))
    return np.stack(rows)

@@ -1,0 +1,397 @@
+import math
+from contextlib import ExitStack
+
+import concourse.mybir as mybir
+from concourse.masks import make_identity
+
+F32 = mybir.dt.float32
+BF16 = mybir.dt.bfloat16
+I32 = mybir.dt.int32
+U32 = mybir.dt.uint32
+U8 = mybir.dt.uint8
+FP8X4 = mybir.dt.float8_e4m3fn_x4
+ALU = mybir.AluOpType
+ACT = mybir.ActivationFunctionType
+AXIS = mybir.AxisListType
+
+P = 128
+B, LQ, LK, DIN, H = 2, 2048, 1024, 1024, 512
+FLOOR = 1e-9
+LARGEST = 3.0e38
+INV_SQRT_H = 1.0 / math.sqrt(H)
+BANK = 512
+
+Q_TILES = LQ // P
+PAIRS_PER_BATCH = Q_TILES // 2
+PAIRS = B * PAIRS_PER_BATCH
+CHUNKS = PAIRS // 2
+
+RING = 12
+LOGS_PER_STEP = 3
+LOG_STEPS = RING // LOGS_PER_STEP
+LAG = 4
+LATE_LOG_STEP = LAG + PAIRS - RING
+
+FLOPS = 2 * B * (LK * DIN * H + 2 * LQ * LK * H)
+
+
+def tile_pgwcrossattention_pa_t_kernel(
+    tc, q, k, v_ret, pi_star, Wv_words, Wv_scales, bv, gamma, out
+):
+    nc = tc.nc
+    with ExitStack() as ctx:
+        consts = ctx.enter_context(tc.tile_pool(name="consts", bufs=1))
+        rows = ctx.enter_context(tc.tile_pool(name="rows", bufs=1))
+        turned = ctx.enter_context(tc.tile_pool(name="turned", bufs=2))
+        logits = ctx.enter_context(tc.tile_pool(name="logits", bufs=RING))
+        packs = ctx.enter_context(tc.tile_pool(name="packs", bufs=2))
+        stats = ctx.enter_context(tc.tile_pool(name="stats", bufs=8))
+        score_banks = ctx.enter_context(tc.psum_pool(name="score_banks", bufs=4))
+        turn_banks = ctx.enter_context(tc.psum_pool(name="turn_banks", bufs=2))
+        sum_banks = ctx.enter_context(tc.psum_pool(name="sum_banks", bufs=2))
+        ctx.enter_context(tc.manual_schedule())
+
+        q_view = [q[b].rearrange("(p t) h -> p t h", t=Q_TILES) for b in range(B)]
+        pi_view = [pi_star[b].rearrange("(p t) c -> p t c", t=Q_TILES) for b in range(B)]
+        out_view = [out[b].rearrange("(p t) h -> p t h", t=Q_TILES) for b in range(B)]
+        k_view = [k[b].rearrange("(t p) h -> p t h", p=P) for b in range(B)]
+        v_view = [
+            v_ret[b].rearrange("(g u p e) d -> g p u (e d)", g=2, u=2, p=P, e=2)
+            for b in range(B)
+        ]
+
+        w_scales = consts.tile([P, 2, H], U8, align_bytes=64)
+        nc.vector.memset(w_scales[:].rearrange("p d n -> p (d n)").bitcast(I32), 0)
+        ident = consts.tile([P, P], F32)
+        make_identity(nc, ident[:])
+        gamma_bf = consts.tile([P, 1], BF16)
+        nc.sync.dma_start(out=gamma_bf[:], in_=gamma.partition_broadcast(P))
+        gain = consts.tile([P, 1], F32)
+        nc.vector.tensor_scalar_mul(out=gain[:], in0=gamma_bf[:], scalar1=math.sqrt(H))
+        w_codes = consts.tile([P, 2, H], U32, align_bytes=64)
+        bias_rows = consts.tile([P, H], BF16)
+        v_codes = [
+            consts.tile([P, 2, H], U32, name="v_codes%d" % b, align_bytes=64)
+            for b in range(B)
+        ]
+        v_scales = [
+            consts.tile([P, 2, H], U8, name="v_scales%d" % b, align_bytes=64)
+            for b in range(B)
+        ]
+
+        key_rows = {}
+        keysT = {}
+        query_rows = {}
+        queriesT = {}
+        plan_rows = {}
+        value_rows = {}
+        value_in = {}
+        z = {}
+        row_max = {}
+        shift = {}
+        row_sum = {}
+        weights = {}
+        weight_banks = {}
+        grouped = {}
+        packed = {}
+        sums = {}
+
+        def load_weight():
+            for quad in range(4):
+                for d in range(2):
+                    nc.sync.dma_start(
+                        out=w_scales[32 * quad : 32 * quad + 4, d, :].bitcast(I32),
+                        in_=Wv_scales[d, 4 * quad : 4 * quad + 4, :].bitcast(I32),
+                    )
+            for d in range(2):
+                nc.sync.dma_start(
+                    out=w_codes[:, d, :].bitcast(I32),
+                    in_=Wv_words[d].rearrange("p n t -> p (n t)").bitcast(I32),
+                )
+            nc.sync.dma_start(out=bias_rows[:], in_=bv.partition_broadcast(P))
+
+        def load_keys(b, half):
+            if half == 0:
+                key_rows[b] = rows.tile([P, LK // P, H], BF16, tag="key_rows", name="key_rows")
+            tiles = slice(4 * half, 4 * half + 4)
+            nc.sync.dma_start(out=key_rows[b][:, tiles, :], in_=k_view[b][:, tiles, :])
+
+        def transpose_keys(b, half):
+            if half == 0:
+                keysT[b] = turned.tile([P, 2, LK], F32, tag="keysT", name="keysT")
+            words = key_rows[b][:].bitcast(F32)
+            for w in range(2):
+                bank = turn_banks.tile([P, BANK], F32, tag="bank")
+                for i in range(4):
+                    nc.tensor.transpose(
+                        bank[:, P * i : P * (i + 1)],
+                        words[:, 4 * half + i, P * w : P * (w + 1)],
+                        ident[:],
+                    )
+                nc.vector.tensor_copy(
+                    out=keysT[b][:, w, BANK * half : BANK * (half + 1)], in_=bank[:]
+                )
+
+        def load_queries(c):
+            b, t0 = c // 4, 4 * (c % 4)
+            query_rows[c] = rows.tile([P, 4, H], BF16, tag="query_rows", name="query_rows", bufs=2)
+            nc.sync.dma_start(out=query_rows[c][:], in_=q_view[b][:, t0 : t0 + 4, :])
+
+        def transpose_queries(c):
+            queriesT[c] = turned.tile([P, 2, BANK], F32, tag="queriesT", name="queriesT")
+            words = query_rows[c][:].bitcast(F32)
+            for w in range(2):
+                bank = turn_banks.tile([P, BANK], F32, tag="bank")
+                for j in range(4):
+                    nc.tensor.transpose(
+                        bank[:, P * j : P * (j + 1)],
+                        words[:, j, P * w : P * (w + 1)],
+                        ident[:],
+                    )
+                nc.scalar.copy(out=queriesT[c][:, w, :], in_=bank[:])
+
+        def load_plan(u):
+            b, t0 = u // PAIRS_PER_BATCH, 2 * (u % PAIRS_PER_BATCH)
+            plan_rows[u] = rows.tile([P, 2, LK], BF16, tag="plan_rows", name="plan_rows", bufs=3)
+            nc.scalar.dma_start(out=plan_rows[u][:], in_=pi_view[b][:, t0 : t0 + 2, :])
+
+        def log_prior(u):
+            z[u] = logits.tile([P, 2, LK], F32, tag="z", name="z")
+            flat = z[u][:].rearrange("p i c -> p (i c)")
+            nc.gpsimd.tensor_scalar(
+                out=flat,
+                in0=plan_rows[u][:].rearrange("p i c -> p (i c)"),
+                scalar1=LARGEST,
+                scalar2=FLOOR,
+                op0=ALU.min,
+                op1=ALU.max,
+            )
+            if u + 3 < PAIRS:
+                load_plan(u + 3)
+            nc.scalar.activation(out=flat, in_=flat, func=ACT.Ln)
+
+        def scores(u, i):
+            b, c = u // PAIRS_PER_BATCH, u // 2
+            j = 2 * (u % 2) + i
+            q_halves = queriesT[c][:].bitcast(BF16).rearrange("p w (c e) -> p w c e", e=2)
+            k_halves = keysT[b][:].bitcast(BF16).rearrange("p w (c e) -> p w c e", e=2)
+            if i == 0:
+                row_max[u] = stats.tile([P, 2], F32, tag="row_max", name="row_max")
+            for n in range(2):
+                bank = score_banks.tile([P, BANK], F32, tag="bank")
+                for w in range(2):
+                    for e in range(2):
+                        nc.tensor.matmul(
+                            out=bank[:],
+                            lhsT=q_halves[:, w, P * j : P * (j + 1), e],
+                            rhs=k_halves[:, w, BANK * n : BANK * (n + 1), e],
+                            start=(w == 0 and e == 0),
+                            stop=(w == 1 and e == 1),
+                        )
+                cols = z[u][:, i, BANK * n : BANK * (n + 1)]
+                nc.vector.scalar_tensor_tensor(
+                    out=cols, in0=cols, scalar=gain[:, 0:1], in1=bank[:], op0=ALU.mult, op1=ALU.add
+                )
+            nc.vector.tensor_reduce(
+                out=row_max[u][:, i : i + 1], in_=z[u][:, i, :], axis=AXIS.X, op=ALU.max
+            )
+            if i == 1:
+                shift[u] = stats.tile([P, 2], F32, tag="shift", name="shift")
+                nc.vector.tensor_scalar_mul(out=shift[u][:], in0=row_max[u][:], scalar1=-INV_SQRT_H)
+
+        def exponentials(u):
+            weights[u] = packs.tile([P, 2, LK], BF16, tag="weights", name="weights", bufs=3)
+            row_sum[u] = stats.tile([P, 2], F32, tag="row_sum", name="row_sum")
+            for i in range(2):
+                nc.scalar.activation(
+                    out=weights[u][:, i, :],
+                    in_=z[u][:, i, :],
+                    func=ACT.Exp,
+                    bias=shift[u][:, i : i + 1],
+                    scale=INV_SQRT_H,
+                    accum_out=row_sum[u][:, i : i + 1],
+                )
+
+        def transpose_weights(u):
+            words = weights[u][:].bitcast(F32)
+            weight_banks[u] = []
+            for i in range(2):
+                bank = turn_banks.tile([P, BANK], F32, tag="bank")
+                for c in range(4):
+                    nc.tensor.transpose(
+                        bank[:, P * c : P * (c + 1)], words[:, i, P * c : P * (c + 1)], ident[:]
+                    )
+                weight_banks[u].append(bank)
+
+        def regroup_weights(u):
+            grouped[u] = packs.tile([P, 2, LK], BF16, tag="grouped", name="grouped", align_bytes=64)
+            words = grouped[u][:].bitcast(F32)
+            for i in range(2):
+                nc.scalar.copy(
+                    out=words[:, i, :].rearrange("p (g c u) -> p g c u", g=2, u=2),
+                    in_=weight_banks[u][i][:].rearrange("p (g u c) -> p g c u", g=2, u=2),
+                )
+
+        def quantise_weights(u):
+            codes = packs.tile([P, 2 * 2 * P], U32, tag="e_codes", align_bytes=64)
+            scales = packs.tile([P, 2 * 2 * P], U8, tag="e_scales", align_bytes=64)
+            nc.vector.quantize_mx(
+                out=codes[:].bitcast(FP8X4),
+                scales=scales[:],
+                in_=grouped[u][:].rearrange("p i c -> p (i c)"),
+            )
+            packed[u] = (codes, scales)
+
+        def weighted_sums(u):
+            b = u // PAIRS_PER_BATCH
+            codes, scales = packed[u]
+            sums[u] = []
+            for i in range(2):
+                bank = sum_banks.tile([P, BANK], F32, tag="bank")
+                for g in range(2):
+                    cols = slice(P * (2 * i + g), P * (2 * i + g + 1))
+                    nc.tensor.matmul_mx(
+                        out=bank[:],
+                        lhsT=codes[:, cols].bitcast(FP8X4),
+                        lhsT_scale=scales[:, cols],
+                        rhs=v_codes[b][:, g, :].bitcast(FP8X4),
+                        rhs_scale=v_scales[b][:, g, :],
+                        start=(g == 0),
+                        stop=(g == 1),
+                    )
+                sums[u].append(bank)
+
+        def normalise(u):
+            b, t0 = u // PAIRS_PER_BATCH, 2 * (u % PAIRS_PER_BATCH)
+            inv_sum = stats.tile([P, 2], F32, tag="inv_sum")
+            nc.vector.reciprocal(out=inv_sum[:], in_=row_sum[u][:])
+            result = packs.tile([P, 2, H], F32, tag="result")
+            nc.vector.tensor_scalar(
+                out=result[:, 0, :], in0=sums[u][0][:], scalar1=inv_sum[:, 0:1], scalar2=None,
+                op0=ALU.mult,
+            )
+            nc.scalar.activation(
+                out=result[:, 1, :], in_=sums[u][1][:], func=ACT.Copy, scale=inv_sum[:, 1:2]
+            )
+            nc.sync.dma_start(out=out_view[b][:, t0 : t0 + 2, :], in_=result[:])
+
+        def load_values(n):
+            b, g = n // 2, n % 2
+            value_rows[n] = rows.tile([P, 4, DIN], BF16, tag="value_rows", name="value_rows")
+            nc.sync.dma_start(
+                out=value_rows[n][:].rearrange("p (u e) d -> p u (e d)", u=2), in_=v_view[b][g]
+            )
+
+        def quantise_values_in(n):
+            words = value_rows[n][:].bitcast(F32)
+            lined = packs.tile([P, 2, 4 * BANK], BF16, tag="v_in_grouped", bufs=1, align_bytes=64)
+            lined_words = lined[:].bitcast(F32).rearrange("p d (c u) -> p d c u", u=2)
+            for t in range(4):
+                bank = turn_banks.tile([P, BANK], F32, tag="bank")
+                for d in range(2):
+                    for u in range(2):
+                        col = P * (2 * d + u)
+                        nc.tensor.transpose(
+                            bank[:, col : col + P],
+                            words[:, t, 256 * d + u : 256 * (d + 1) : 2],
+                            ident[:],
+                        )
+                nc.vector.tensor_copy(
+                    out=lined_words[:, :, P * t : P * (t + 1), :],
+                    in_=bank[:].rearrange("p (d u c) -> p d c u", d=2, u=2),
+                )
+            codes = packs.tile([P, 2, BANK], U32, tag="v_in_codes", bufs=1, align_bytes=64)
+            scales = packs.tile([P, 2, BANK], U8, tag="v_in_scales", bufs=1, align_bytes=64)
+            nc.vector.quantize_mx(
+                out=codes[:].rearrange("p d c -> p (d c)").bitcast(FP8X4),
+                scales=scales[:].rearrange("p d c -> p (d c)"),
+                in_=lined[:].rearrange("p d c -> p (d c)"),
+            )
+            value_in[n] = (codes, scales)
+
+        def project_values(n):
+            b, g = n // 2, n % 2
+            codes, scales = value_in[n]
+            lined = packs.tile([P, 4 * H], BF16, tag="v_grouped", bufs=1, align_bytes=64)
+            for hb in range(4):
+                h_cols = slice(P * hb, P * (hb + 1))
+                bank = sum_banks.tile([P, BANK], F32, tag="bank")
+                for t in range(4):
+                    t_cols = slice(P * t, P * (t + 1))
+                    for d in range(2):
+                        nc.tensor.matmul_mx(
+                            out=bank[:, t_cols],
+                            lhsT=codes[:, d, t_cols].bitcast(FP8X4),
+                            lhsT_scale=scales[:, d, t_cols],
+                            rhs=w_codes[:, d, h_cols].bitcast(FP8X4),
+                            rhs_scale=w_scales[:, d, h_cols],
+                            start=(d == 0),
+                            stop=(d == 1),
+                        )
+                nc.vector.tensor_tensor(
+                    out=lined[:, 4 * P * hb : 4 * P * (hb + 1)].rearrange("p (h t) -> p h t", t=4),
+                    in0=bank[:].rearrange("p (t h) -> p h t", t=4),
+                    in1=bias_rows[:, h_cols].unsqueeze(2).to_broadcast([P, P, 4]),
+                    op=ALU.add,
+                )
+            nc.vector.quantize_mx(
+                out=v_codes[b][:, g, :].bitcast(FP8X4), scales=v_scales[b][:, g, :], in_=lined[:]
+            )
+
+        for u in range(3):
+            load_plan(u)
+        load_keys(0, 0)
+        load_queries(0)
+        load_keys(0, 1)
+        load_queries(1)
+        load_weight()
+        load_values(0)
+        transpose_keys(0, 0)
+        transpose_queries(0)
+        load_queries(2)
+        transpose_keys(0, 1)
+        load_keys(1, 0)
+        load_keys(1, 1)
+
+        for s in range(PAIRS + LAG + 4):
+            exped, turning, summing = s - LAG, s - LAG - 2, s - LAG - 3
+            if s < LOG_STEPS:
+                for u in range(LOGS_PER_STEP * s, LOGS_PER_STEP * (s + 1)):
+                    log_prior(u)
+            if s == LATE_LOG_STEP:
+                for u in range(RING, PAIRS):
+                    log_prior(u)
+            if 0 <= summing < PAIRS:
+                quantise_weights(summing)
+            if 0 <= turning < PAIRS:
+                transpose_weights(turning)
+            if 0 <= exped < PAIRS:
+                exponentials(exped)
+            if 0 <= turning < PAIRS:
+                regroup_weights(turning)
+            if s < PAIRS:
+                scores(s, 0)
+            if 0 <= summing < PAIRS:
+                weighted_sums(summing)
+            if s < PAIRS:
+                scores(s, 1)
+            if 0 <= summing < PAIRS:
+                normalise(summing)
+            if s < PAIRS:
+                in_batch = s % PAIRS_PER_BATCH
+                if in_batch < 4:
+                    n = 2 * (s // PAIRS_PER_BATCH) + in_batch // 2
+                    if in_batch % 2 == 0:
+                        quantise_values_in(n)
+                        if n + 1 < 2 * B:
+                            load_values(n + 1)
+                    else:
+                        project_values(n)
+                if s % 2 == 1 and (s + 1) // 2 < CHUNKS:
+                    transpose_queries((s + 1) // 2)
+                    if (s + 1) // 2 + 2 < CHUNKS:
+                        load_queries((s + 1) // 2 + 2)
+                if s == PAIRS_PER_BATCH - 2:
+                    transpose_keys(1, 0)
+                if s == PAIRS_PER_BATCH - 1:
+                    transpose_keys(1, 1)

@@ -17,7 +17,6 @@ AXIS = mybir.AxisListType
 P = 128
 B, LQ, LK, DIN, H = 2, 2048, 1024, 1024, 512
 FLOOR = 1e-9
-LARGEST = 3.0e38
 INV_SQRT_H = 1.0 / math.sqrt(H)
 BANK = 512
 
@@ -27,10 +26,9 @@ PAIRS = B * PAIRS_PER_BATCH
 CHUNKS = PAIRS // 2
 
 RING = 12
-LOGS_PER_STEP = 3
-LOG_STEPS = RING // LOGS_PER_STEP
-LAG = 4
-LATE_LOG_STEP = LAG + PAIRS - RING
+LOGS_PER_ROUND = 2
+FIRST_ATTEND = 6
+MOST_ATTENDS = 2
 
 FLOPS = 2 * B * (LK * DIN * H + 2 * LQ * LK * H)
 
@@ -49,7 +47,6 @@ def tile_pgwcrossattention_pa_t_kernel(
         score_banks = ctx.enter_context(tc.psum_pool(name="score_banks", bufs=4))
         turn_banks = ctx.enter_context(tc.psum_pool(name="turn_banks", bufs=2))
         sum_banks = ctx.enter_context(tc.psum_pool(name="sum_banks", bufs=2))
-        ctx.enter_context(tc.manual_schedule())
 
         q_view = [q[b].rearrange("(p t) h -> p t h", t=Q_TILES) for b in range(B)]
         pi_view = [pi_star[b].rearrange("(p t) c -> p t c", t=Q_TILES) for b in range(B)]
@@ -158,13 +155,8 @@ def tile_pgwcrossattention_pa_t_kernel(
         def log_prior(u):
             z[u] = logits.tile([P, 2, LK], F32, tag="z", name="z")
             flat = z[u][:].rearrange("p i c -> p (i c)")
-            nc.gpsimd.tensor_scalar(
-                out=flat,
-                in0=plan_rows[u][:].rearrange("p i c -> p (i c)"),
-                scalar1=LARGEST,
-                scalar2=FLOOR,
-                op0=ALU.min,
-                op1=ALU.max,
+            nc.vector.tensor_scalar_max(
+                out=flat, in0=plan_rows[u][:].rearrange("p i c -> p (i c)"), scalar1=FLOOR
             )
             if u + 3 < PAIRS:
                 load_plan(u + 3)
@@ -296,7 +288,7 @@ def tile_pgwcrossattention_pa_t_kernel(
                             words[:, t, 256 * d + u : 256 * (d + 1) : 2],
                             ident[:],
                         )
-                nc.vector.tensor_copy(
+                nc.scalar.copy(
                     out=lined_words[:, :, P * t : P * (t + 1), :],
                     in_=bank[:].rearrange("p (d u c) -> p d c u", d=2, u=2),
                 )
@@ -353,45 +345,62 @@ def tile_pgwcrossattention_pa_t_kernel(
         load_keys(1, 0)
         load_keys(1, 1)
 
-        for s in range(PAIRS + LAG + 4):
-            exped, turning, summing = s - LAG, s - LAG - 2, s - LAG - 3
-            if s < LOG_STEPS:
-                for u in range(LOGS_PER_STEP * s, LOGS_PER_STEP * (s + 1)):
+        def attend_front(x):
+            if 0 <= x - 2 < PAIRS:
+                quantise_weights(x - 2)
+            if 0 <= x - 1 < PAIRS:
+                transpose_weights(x - 1)
+            if x < PAIRS:
+                exponentials(x)
+            if 0 <= x - 1 < PAIRS:
+                regroup_weights(x - 1)
+
+        def attend_back(x):
+            if 0 <= x - 2 < PAIRS:
+                weighted_sums(x - 2)
+                normalise(x - 2)
+
+        x = 0
+        logged = 0
+        for r in range(PAIRS):
+            if logged < RING:
+                for u in range(logged, min(RING, logged + LOGS_PER_ROUND)):
                     log_prior(u)
-            if s == LATE_LOG_STEP:
-                for u in range(RING, PAIRS):
+                logged = min(RING, logged + LOGS_PER_ROUND)
+            elif logged < PAIRS and x >= PAIRS - RING:
+                for u in range(logged, PAIRS):
                     log_prior(u)
-            if 0 <= summing < PAIRS:
-                quantise_weights(summing)
-            if 0 <= turning < PAIRS:
-                transpose_weights(turning)
-            if 0 <= exped < PAIRS:
-                exponentials(exped)
-            if 0 <= turning < PAIRS:
-                regroup_weights(turning)
-            if s < PAIRS:
-                scores(s, 0)
-            if 0 <= summing < PAIRS:
-                weighted_sums(summing)
-            if s < PAIRS:
-                scores(s, 1)
-            if 0 <= summing < PAIRS:
-                normalise(summing)
-            if s < PAIRS:
-                in_batch = s % PAIRS_PER_BATCH
-                if in_batch < 4:
-                    n = 2 * (s // PAIRS_PER_BATCH) + in_batch // 2
-                    if in_batch % 2 == 0:
-                        quantise_values_in(n)
-                        if n + 1 < 2 * B:
-                            load_values(n + 1)
-                    else:
-                        project_values(n)
-                if s % 2 == 1 and (s + 1) // 2 < CHUNKS:
-                    transpose_queries((s + 1) // 2)
-                    if (s + 1) // 2 + 2 < CHUNKS:
-                        load_queries((s + 1) // 2 + 2)
-                if s == PAIRS_PER_BATCH - 2:
-                    transpose_keys(1, 0)
-                if s == PAIRS_PER_BATCH - 1:
-                    transpose_keys(1, 1)
+                logged = PAIRS
+            attends = 0 if r < FIRST_ATTEND else min(MOST_ATTENDS, r - x)
+            if attends > 0:
+                attend_front(x)
+            scores(r, 0)
+            if attends > 0:
+                attend_back(x)
+                x += 1
+            if attends > 1:
+                attend_front(x)
+            scores(r, 1)
+            if attends > 1:
+                attend_back(x)
+                x += 1
+            if r < 4 * B:
+                n, part = r // 2, r % 2
+                if part == 0:
+                    quantise_values_in(n)
+                    if n + 1 < 2 * B:
+                        load_values(n + 1)
+                else:
+                    project_values(n)
+            if r % 2 == 1 and (r + 1) // 2 < CHUNKS:
+                transpose_queries((r + 1) // 2)
+                if (r + 1) // 2 + 2 < CHUNKS:
+                    load_queries((r + 1) // 2 + 2)
+            if r == PAIRS_PER_BATCH - 2:
+                transpose_keys(1, 0)
+            if r == PAIRS_PER_BATCH - 1:
+                transpose_keys(1, 1)
+        while x < PAIRS + 2:
+            attend_front(x)
+            attend_back(x)
+            x += 1

@@ -19,16 +19,22 @@ B, LQ, LK, DIN, H = 2, 2048, 1024, 1024, 512
 FLOOR = 1e-9
 INV_SQRT_H = 1.0 / math.sqrt(H)
 BANK = 512
+K_PASS = 4 * P
+GROUPS = LK // K_PASS
 
 Q_TILES = LQ // P
+KEY_TILES = LK // P
 PAIRS_PER_BATCH = Q_TILES // 2
 PAIRS = B * PAIRS_PER_BATCH
-CHUNKS = PAIRS // 2
+CHUNK = 4
+CHUNKS = B * Q_TILES // CHUNK
+HALVES = B * GROUPS
 
 RING = 12
 LOGS_PER_ROUND = 2
-FIRST_ATTEND = 6
+FIRST_ATTEND = RING // LOGS_PER_ROUND
 MOST_ATTENDS = 2
+PLANS_AHEAD = 3
 
 FLOPS = 2 * B * (LK * DIN * H + 2 * LQ * LK * H)
 
@@ -43,7 +49,7 @@ def tile_pgwcrossattention_pa_t_kernel(
         turned = ctx.enter_context(tc.tile_pool(name="turned", bufs=2))
         logits = ctx.enter_context(tc.tile_pool(name="logits", bufs=RING))
         packs = ctx.enter_context(tc.tile_pool(name="packs", bufs=2))
-        stats = ctx.enter_context(tc.tile_pool(name="stats", bufs=8))
+        stats = ctx.enter_context(tc.tile_pool(name="stats", bufs=FIRST_ATTEND + 2))
         score_banks = ctx.enter_context(tc.psum_pool(name="score_banks", bufs=4))
         turn_banks = ctx.enter_context(tc.psum_pool(name="turn_banks", bufs=2))
         sum_banks = ctx.enter_context(tc.psum_pool(name="sum_banks", bufs=2))
@@ -53,11 +59,11 @@ def tile_pgwcrossattention_pa_t_kernel(
         out_view = [out[b].rearrange("(p t) h -> p t h", t=Q_TILES) for b in range(B)]
         k_view = [k[b].rearrange("(t p) h -> p t h", p=P) for b in range(B)]
         v_view = [
-            v_ret[b].rearrange("(g u p e) d -> g p u (e d)", g=2, u=2, p=P, e=2)
+            v_ret[b].rearrange("(g u p i) d -> g p u (i d)", g=GROUPS, u=2, p=P, i=2)
             for b in range(B)
         ]
 
-        w_scales = consts.tile([P, 2, H], U8, align_bytes=64)
+        w_scales = consts.tile([P, GROUPS, H], U8, align_bytes=64)
         nc.vector.memset(w_scales[:].rearrange("p d n -> p (d n)").bitcast(I32), 0)
         ident = consts.tile([P, P], F32)
         make_identity(nc, ident[:])
@@ -65,14 +71,14 @@ def tile_pgwcrossattention_pa_t_kernel(
         nc.sync.dma_start(out=gamma_bf[:], in_=gamma.partition_broadcast(P))
         gain = consts.tile([P, 1], F32)
         nc.vector.tensor_scalar_mul(out=gain[:], in0=gamma_bf[:], scalar1=math.sqrt(H))
-        w_codes = consts.tile([P, 2, H], U32, align_bytes=64)
+        w_codes = consts.tile([P, GROUPS, H], U32, align_bytes=64)
         bias_rows = consts.tile([P, H], BF16)
         v_codes = [
-            consts.tile([P, 2, H], U32, name="v_codes%d" % b, align_bytes=64)
+            consts.tile([P, GROUPS, H], U32, name="v_codes%d" % b, align_bytes=64)
             for b in range(B)
         ]
         v_scales = [
-            consts.tile([P, 2, H], U8, name="v_scales%d" % b, align_bytes=64)
+            consts.tile([P, GROUPS, H], U8, name="v_scales%d" % b, align_bytes=64)
             for b in range(B)
         ]
 
@@ -87,20 +93,20 @@ def tile_pgwcrossattention_pa_t_kernel(
         row_max = {}
         shift = {}
         row_sum = {}
+        inv_sum = {}
         weights = {}
         weight_banks = {}
         grouped = {}
         packed = {}
-        sums = {}
 
         def load_weight():
             for quad in range(4):
-                for d in range(2):
+                for d in range(GROUPS):
                     nc.sync.dma_start(
                         out=w_scales[32 * quad : 32 * quad + 4, d, :].bitcast(I32),
                         in_=Wv_scales[d, 4 * quad : 4 * quad + 4, :].bitcast(I32),
                     )
-            for d in range(2):
+            for d in range(GROUPS):
                 nc.sync.dma_start(
                     out=w_codes[:, d, :].bitcast(I32),
                     in_=Wv_words[d].rearrange("p n t -> p (n t)").bitcast(I32),
@@ -109,7 +115,7 @@ def tile_pgwcrossattention_pa_t_kernel(
 
         def load_keys(b, half):
             if half == 0:
-                key_rows[b] = rows.tile([P, LK // P, H], BF16, tag="key_rows", name="key_rows")
+                key_rows[b] = rows.tile([P, KEY_TILES, H], BF16, tag="key_rows", name="key_rows")
             tiles = slice(4 * half, 4 * half + 4)
             nc.sync.dma_start(out=key_rows[b][:, tiles, :], in_=k_view[b][:, tiles, :])
 
@@ -130,16 +136,18 @@ def tile_pgwcrossattention_pa_t_kernel(
                 )
 
         def load_queries(c):
-            b, t0 = c // 4, 4 * (c % 4)
-            query_rows[c] = rows.tile([P, 4, H], BF16, tag="query_rows", name="query_rows", bufs=2)
-            nc.sync.dma_start(out=query_rows[c][:], in_=q_view[b][:, t0 : t0 + 4, :])
+            b, t0 = c // (CHUNKS // B), CHUNK * (c % (CHUNKS // B))
+            query_rows[c] = rows.tile(
+                [P, CHUNK, H], BF16, tag="query_rows", name="query_rows", bufs=2
+            )
+            nc.sync.dma_start(out=query_rows[c][:], in_=q_view[b][:, t0 : t0 + CHUNK, :])
 
         def transpose_queries(c):
-            queriesT[c] = turned.tile([P, 2, BANK], F32, tag="queriesT", name="queriesT")
+            queriesT[c] = turned.tile([P, 2, CHUNK * P], F32, tag="queriesT", name="queriesT")
             words = query_rows[c][:].bitcast(F32)
             for w in range(2):
                 bank = turn_banks.tile([P, BANK], F32, tag="bank")
-                for j in range(4):
+                for j in range(CHUNK):
                     nc.tensor.transpose(
                         bank[:, P * j : P * (j + 1)],
                         words[:, j, P * w : P * (w + 1)],
@@ -149,7 +157,9 @@ def tile_pgwcrossattention_pa_t_kernel(
 
         def load_plan(u):
             b, t0 = u // PAIRS_PER_BATCH, 2 * (u % PAIRS_PER_BATCH)
-            plan_rows[u] = rows.tile([P, 2, LK], BF16, tag="plan_rows", name="plan_rows", bufs=3)
+            plan_rows[u] = rows.tile(
+                [P, 2, LK], BF16, tag="plan_rows", name="plan_rows", bufs=PLANS_AHEAD
+            )
             nc.scalar.dma_start(out=plan_rows[u][:], in_=pi_view[b][:, t0 : t0 + 2, :])
 
         def log_prior(u):
@@ -158,8 +168,8 @@ def tile_pgwcrossattention_pa_t_kernel(
             nc.vector.tensor_scalar_max(
                 out=flat, in0=plan_rows[u][:].rearrange("p i c -> p (i c)"), scalar1=FLOOR
             )
-            if u + 3 < PAIRS:
-                load_plan(u + 3)
+            if u + PLANS_AHEAD < PAIRS:
+                load_plan(u + PLANS_AHEAD)
             nc.scalar.activation(out=flat, in_=flat, func=ACT.Ln)
 
         def scores(u, i):
@@ -169,7 +179,7 @@ def tile_pgwcrossattention_pa_t_kernel(
             k_halves = keysT[b][:].bitcast(BF16).rearrange("p w (c e) -> p w c e", e=2)
             if i == 0:
                 row_max[u] = stats.tile([P, 2], F32, tag="row_max", name="row_max")
-            for n in range(2):
+            for n in range(LK // BANK):
                 bank = score_banks.tile([P, BANK], F32, tag="bank")
                 for w in range(2):
                     for e in range(2):
@@ -189,7 +199,9 @@ def tile_pgwcrossattention_pa_t_kernel(
             )
             if i == 1:
                 shift[u] = stats.tile([P, 2], F32, tag="shift", name="shift")
-                nc.vector.tensor_scalar_mul(out=shift[u][:], in0=row_max[u][:], scalar1=-INV_SQRT_H)
+                nc.vector.tensor_scalar_mul(
+                    out=shift[u][:], in0=row_max[u][:], scalar1=-INV_SQRT_H
+                )
 
         def exponentials(u):
             weights[u] = packs.tile([P, 2, LK], BF16, tag="weights", name="weights", bufs=3)
@@ -220,28 +232,30 @@ def tile_pgwcrossattention_pa_t_kernel(
             words = grouped[u][:].bitcast(F32)
             for i in range(2):
                 nc.scalar.copy(
-                    out=words[:, i, :].rearrange("p (g c u) -> p g c u", g=2, u=2),
-                    in_=weight_banks[u][i][:].rearrange("p (g u c) -> p g c u", g=2, u=2),
+                    out=words[:, i, :].rearrange("p (g c u) -> p g c u", g=GROUPS, u=2),
+                    in_=weight_banks[u][i][:].rearrange("p (g u c) -> p g c u", g=GROUPS, u=2),
                 )
 
         def quantise_weights(u):
-            codes = packs.tile([P, 2 * 2 * P], U32, tag="e_codes", align_bytes=64)
-            scales = packs.tile([P, 2 * 2 * P], U8, tag="e_scales", align_bytes=64)
+            codes = packs.tile([P, 2 * GROUPS * P], U32, tag="e_codes", align_bytes=64)
+            scales = packs.tile([P, 2 * GROUPS * P], U8, tag="e_scales", align_bytes=64)
             nc.vector.quantize_mx(
                 out=codes[:].bitcast(FP8X4),
                 scales=scales[:],
                 in_=grouped[u][:].rearrange("p i c -> p (i c)"),
             )
             packed[u] = (codes, scales)
+            inv_sum[u] = stats.tile([P, 2], F32, tag="inv_sum", name="inv_sum")
+            nc.vector.reciprocal(out=inv_sum[u][:], in_=row_sum[u][:])
 
         def weighted_sums(u):
-            b = u // PAIRS_PER_BATCH
+            b, t0 = u // PAIRS_PER_BATCH, 2 * (u % PAIRS_PER_BATCH)
             codes, scales = packed[u]
-            sums[u] = []
+            sums = []
             for i in range(2):
                 bank = sum_banks.tile([P, BANK], F32, tag="bank")
-                for g in range(2):
-                    cols = slice(P * (2 * i + g), P * (2 * i + g + 1))
+                for g in range(GROUPS):
+                    cols = slice(P * (GROUPS * i + g), P * (GROUPS * i + g + 1))
                     nc.tensor.matmul_mx(
                         out=bank[:],
                         lhsT=codes[:, cols].bitcast(FP8X4),
@@ -249,38 +263,38 @@ def tile_pgwcrossattention_pa_t_kernel(
                         rhs=v_codes[b][:, g, :].bitcast(FP8X4),
                         rhs_scale=v_scales[b][:, g, :],
                         start=(g == 0),
-                        stop=(g == 1),
+                        stop=(g == GROUPS - 1),
                     )
-                sums[u].append(bank)
-
-        def normalise(u):
-            b, t0 = u // PAIRS_PER_BATCH, 2 * (u % PAIRS_PER_BATCH)
-            inv_sum = stats.tile([P, 2], F32, tag="inv_sum")
-            nc.vector.reciprocal(out=inv_sum[:], in_=row_sum[u][:])
+                sums.append(bank)
             result = packs.tile([P, 2, H], F32, tag="result")
             nc.vector.tensor_scalar(
-                out=result[:, 0, :], in0=sums[u][0][:], scalar1=inv_sum[:, 0:1], scalar2=None,
+                out=result[:, 0, :],
+                in0=sums[0][:],
+                scalar1=inv_sum[u][:, 0:1],
+                scalar2=None,
                 op0=ALU.mult,
             )
             nc.scalar.activation(
-                out=result[:, 1, :], in_=sums[u][1][:], func=ACT.Copy, scale=inv_sum[:, 1:2]
+                out=result[:, 1, :], in_=sums[1][:], func=ACT.Copy, scale=inv_sum[u][:, 1:2]
             )
             nc.sync.dma_start(out=out_view[b][:, t0 : t0 + 2, :], in_=result[:])
 
         def load_values(n):
-            b, g = n // 2, n % 2
+            b, g = n // GROUPS, n % GROUPS
             value_rows[n] = rows.tile([P, 4, DIN], BF16, tag="value_rows", name="value_rows")
             nc.sync.dma_start(
-                out=value_rows[n][:].rearrange("p (u e) d -> p u (e d)", u=2), in_=v_view[b][g]
+                out=value_rows[n][:].rearrange("p (u i) d -> p u (i d)", u=2), in_=v_view[b][g]
             )
 
         def quantise_values_in(n):
             words = value_rows[n][:].bitcast(F32)
-            lined = packs.tile([P, 2, 4 * BANK], BF16, tag="v_in_grouped", bufs=1, align_bytes=64)
+            lined = packs.tile(
+                [P, GROUPS, 4 * BANK], BF16, tag="v_in_grouped", bufs=1, align_bytes=64
+            )
             lined_words = lined[:].bitcast(F32).rearrange("p d (c u) -> p d c u", u=2)
             for t in range(4):
                 bank = turn_banks.tile([P, BANK], F32, tag="bank")
-                for d in range(2):
+                for d in range(GROUPS):
                     for u in range(2):
                         col = P * (2 * d + u)
                         nc.tensor.transpose(
@@ -290,10 +304,10 @@ def tile_pgwcrossattention_pa_t_kernel(
                         )
                 nc.scalar.copy(
                     out=lined_words[:, :, P * t : P * (t + 1), :],
-                    in_=bank[:].rearrange("p (d u c) -> p d c u", d=2, u=2),
+                    in_=bank[:].rearrange("p (d u c) -> p d c u", d=GROUPS, u=2),
                 )
-            codes = packs.tile([P, 2, BANK], U32, tag="v_in_codes", bufs=1, align_bytes=64)
-            scales = packs.tile([P, 2, BANK], U8, tag="v_in_scales", bufs=1, align_bytes=64)
+            codes = packs.tile([P, GROUPS, BANK], U32, tag="v_in_codes", bufs=1, align_bytes=64)
+            scales = packs.tile([P, GROUPS, BANK], U8, tag="v_in_scales", bufs=1, align_bytes=64)
             nc.vector.quantize_mx(
                 out=codes[:].rearrange("p d c -> p (d c)").bitcast(FP8X4),
                 scales=scales[:].rearrange("p d c -> p (d c)"),
@@ -302,15 +316,15 @@ def tile_pgwcrossattention_pa_t_kernel(
             value_in[n] = (codes, scales)
 
         def project_values(n):
-            b, g = n // 2, n % 2
+            b, g = n // GROUPS, n % GROUPS
             codes, scales = value_in[n]
             lined = packs.tile([P, 4 * H], BF16, tag="v_grouped", bufs=1, align_bytes=64)
-            for hb in range(4):
+            for hb in range(H // P):
                 h_cols = slice(P * hb, P * (hb + 1))
                 bank = sum_banks.tile([P, BANK], F32, tag="bank")
                 for t in range(4):
                     t_cols = slice(P * t, P * (t + 1))
-                    for d in range(2):
+                    for d in range(GROUPS):
                         nc.tensor.matmul_mx(
                             out=bank[:, t_cols],
                             lhsT=codes[:, d, t_cols].bitcast(FP8X4),
@@ -318,7 +332,7 @@ def tile_pgwcrossattention_pa_t_kernel(
                             rhs=w_codes[:, d, h_cols].bitcast(FP8X4),
                             rhs_scale=w_scales[:, d, h_cols],
                             start=(d == 0),
-                            stop=(d == 1),
+                            stop=(d == GROUPS - 1),
                         )
                 nc.vector.tensor_tensor(
                     out=lined[:, 4 * P * hb : 4 * P * (hb + 1)].rearrange("p (h t) -> p h t", t=4),
@@ -329,21 +343,6 @@ def tile_pgwcrossattention_pa_t_kernel(
             nc.vector.quantize_mx(
                 out=v_codes[b][:, g, :].bitcast(FP8X4), scales=v_scales[b][:, g, :], in_=lined[:]
             )
-
-        for u in range(3):
-            load_plan(u)
-        load_keys(0, 0)
-        load_queries(0)
-        load_keys(0, 1)
-        load_queries(1)
-        load_weight()
-        load_values(0)
-        transpose_keys(0, 0)
-        transpose_queries(0)
-        load_queries(2)
-        transpose_keys(0, 1)
-        load_keys(1, 0)
-        load_keys(1, 1)
 
         def attend_front(x):
             if 0 <= x - 2 < PAIRS:
@@ -358,15 +357,29 @@ def tile_pgwcrossattention_pa_t_kernel(
         def attend_back(x):
             if 0 <= x - 2 < PAIRS:
                 weighted_sums(x - 2)
-                normalise(x - 2)
+
+        for u in range(PLANS_AHEAD):
+            load_plan(u)
+        load_keys(0, 0)
+        load_queries(0)
+        load_keys(0, 1)
+        load_queries(1)
+        load_weight()
+        load_values(0)
+        transpose_keys(0, 0)
+        transpose_queries(0)
+        load_queries(2)
+        transpose_keys(0, 1)
+        load_keys(1, 0)
+        load_keys(1, 1)
 
         x = 0
         logged = 0
         for r in range(PAIRS):
             if logged < RING:
-                for u in range(logged, min(RING, logged + LOGS_PER_ROUND)):
+                for u in range(logged, logged + LOGS_PER_ROUND):
                     log_prior(u)
-                logged = min(RING, logged + LOGS_PER_ROUND)
+                logged += LOGS_PER_ROUND
             elif logged < PAIRS and x >= PAIRS - RING:
                 for u in range(logged, PAIRS):
                     log_prior(u)
@@ -384,22 +397,21 @@ def tile_pgwcrossattention_pa_t_kernel(
             if attends > 1:
                 attend_back(x)
                 x += 1
-            if r < 4 * B:
-                n, part = r // 2, r % 2
-                if part == 0:
+            if r < 2 * HALVES:
+                n = r // 2
+                if r % 2 == 0:
                     quantise_values_in(n)
-                    if n + 1 < 2 * B:
+                    if n + 1 < HALVES:
                         load_values(n + 1)
                 else:
                     project_values(n)
-            if r % 2 == 1 and (r + 1) // 2 < CHUNKS:
-                transpose_queries((r + 1) // 2)
-                if (r + 1) // 2 + 2 < CHUNKS:
-                    load_queries((r + 1) // 2 + 2)
-            if r == PAIRS_PER_BATCH - 2:
-                transpose_keys(1, 0)
-            if r == PAIRS_PER_BATCH - 1:
-                transpose_keys(1, 1)
+            c = (r + 1) // 2
+            if r % 2 == 1 and c < CHUNKS:
+                transpose_queries(c)
+                if c + 2 < CHUNKS:
+                    load_queries(c + 2)
+            if PAIRS_PER_BATCH - 2 <= r < PAIRS_PER_BATCH:
+                transpose_keys(1, r - (PAIRS_PER_BATCH - 2))
         while x < PAIRS + 2:
             attend_front(x)
             attend_back(x)

@@ -19,14 +19,17 @@ B, LQ, LK, DIN, H = 2, 2048, 1024, 1024, 512
 FLOOR = 1e-9
 INV_SQRT_H = 1.0 / math.sqrt(H)
 BANK = 512
+PER_BANK = BANK // P
+QUADRANT = 32
 K_PASS = 4 * P
+PASS_WORDS = K_PASS // 2
 GROUPS = LK // K_PASS
 
 Q_TILES = LQ // P
 KEY_TILES = LK // P
 PAIRS_PER_BATCH = Q_TILES // 2
 PAIRS = B * PAIRS_PER_BATCH
-CHUNK = 4
+CHUNK = PER_BANK
 CHUNKS = B * Q_TILES // CHUNK
 HALVES = B * GROUPS
 
@@ -68,9 +71,7 @@ def tile_pgwcrossattention_pa_t_kernel(
         ident = consts.tile([P, P], F32)
         make_identity(nc, ident[:])
         gamma_bf = consts.tile([P, 1], BF16)
-        nc.sync.dma_start(out=gamma_bf[:], in_=gamma.partition_broadcast(P))
         gain = consts.tile([P, 1], F32)
-        nc.vector.tensor_scalar_mul(out=gain[:], in0=gamma_bf[:], scalar1=math.sqrt(H))
         w_codes = consts.tile([P, GROUPS, H], U32, align_bytes=64)
         bias_rows = consts.tile([P, H], BF16)
         v_codes = [
@@ -99,24 +100,27 @@ def tile_pgwcrossattention_pa_t_kernel(
         grouped = {}
         packed = {}
 
+        def load_gain():
+            nc.sync.dma_start(out=gamma_bf[:], in_=gamma.partition_broadcast(P))
+            nc.vector.tensor_scalar_mul(out=gain[:], in0=gamma_bf[:], scalar1=math.sqrt(H))
+
         def load_weight():
-            for quad in range(4):
-                for d in range(GROUPS):
-                    nc.sync.dma_start(
-                        out=w_scales[32 * quad : 32 * quad + 4, d, :].bitcast(I32),
-                        in_=Wv_scales[d, 4 * quad : 4 * quad + 4, :].bitcast(I32),
-                    )
             for d in range(GROUPS):
                 nc.sync.dma_start(
                     out=w_codes[:, d, :].bitcast(I32),
                     in_=Wv_words[d].rearrange("p n t -> p (n t)").bitcast(I32),
+                )
+            for quad in range(P // QUADRANT):
+                nc.sync.dma_start(
+                    out=w_scales[QUADRANT * quad : QUADRANT * quad + 4, :, :].bitcast(I32),
+                    in_=Wv_scales[:, 4 * quad : 4 * quad + 4, :].rearrange("d r n -> r d n").bitcast(I32),
                 )
             nc.sync.dma_start(out=bias_rows[:], in_=bv.partition_broadcast(P))
 
         def load_keys(b, half):
             if half == 0:
                 key_rows[b] = rows.tile([P, KEY_TILES, H], BF16, tag="key_rows", name="key_rows")
-            tiles = slice(4 * half, 4 * half + 4)
+            tiles = slice(PER_BANK * half, PER_BANK * (half + 1))
             nc.sync.dma_start(out=key_rows[b][:, tiles, :], in_=k_view[b][:, tiles, :])
 
         def transpose_keys(b, half):
@@ -125,10 +129,10 @@ def tile_pgwcrossattention_pa_t_kernel(
             words = key_rows[b][:].bitcast(F32)
             for w in range(2):
                 bank = turn_banks.tile([P, BANK], F32, tag="bank")
-                for i in range(4):
+                for i in range(PER_BANK):
                     nc.tensor.transpose(
                         bank[:, P * i : P * (i + 1)],
-                        words[:, 4 * half + i, P * w : P * (w + 1)],
+                        words[:, PER_BANK * half + i, P * w : P * (w + 1)],
                         ident[:],
                     )
                 nc.vector.tensor_copy(
@@ -221,7 +225,7 @@ def tile_pgwcrossattention_pa_t_kernel(
             weight_banks[u] = []
             for i in range(2):
                 bank = turn_banks.tile([P, BANK], F32, tag="bank")
-                for c in range(4):
+                for c in range(PER_BANK):
                     nc.tensor.transpose(
                         bank[:, P * c : P * (c + 1)], words[:, i, P * c : P * (c + 1)], ident[:]
                     )
@@ -281,7 +285,7 @@ def tile_pgwcrossattention_pa_t_kernel(
 
         def load_values(n):
             b, g = n // GROUPS, n % GROUPS
-            value_rows[n] = rows.tile([P, 4, DIN], BF16, tag="value_rows", name="value_rows")
+            value_rows[n] = rows.tile([P, PER_BANK, DIN], BF16, tag="value_rows", name="value_rows")
             nc.sync.dma_start(
                 out=value_rows[n][:].rearrange("p (u i) d -> p u (i d)", u=2), in_=v_view[b][g]
             )
@@ -292,14 +296,14 @@ def tile_pgwcrossattention_pa_t_kernel(
                 [P, GROUPS, 4 * BANK], BF16, tag="v_in_grouped", bufs=1, align_bytes=64
             )
             lined_words = lined[:].bitcast(F32).rearrange("p d (c u) -> p d c u", u=2)
-            for t in range(4):
+            for t in range(PER_BANK):
                 bank = turn_banks.tile([P, BANK], F32, tag="bank")
                 for d in range(GROUPS):
                     for u in range(2):
                         col = P * (2 * d + u)
                         nc.tensor.transpose(
                             bank[:, col : col + P],
-                            words[:, t, 256 * d + u : 256 * (d + 1) : 2],
+                            words[:, t, PASS_WORDS * d + u : PASS_WORDS * (d + 1) : 2],
                             ident[:],
                         )
                 nc.scalar.copy(
@@ -322,7 +326,7 @@ def tile_pgwcrossattention_pa_t_kernel(
             for hb in range(H // P):
                 h_cols = slice(P * hb, P * (hb + 1))
                 bank = sum_banks.tile([P, BANK], F32, tag="bank")
-                for t in range(4):
+                for t in range(PER_BANK):
                     t_cols = slice(P * t, P * (t + 1))
                     for d in range(GROUPS):
                         nc.tensor.matmul_mx(
@@ -362,10 +366,11 @@ def tile_pgwcrossattention_pa_t_kernel(
             load_plan(u)
         load_keys(0, 0)
         load_queries(0)
+        load_gain()
         load_keys(0, 1)
         load_queries(1)
-        load_weight()
         load_values(0)
+        load_weight()
         transpose_keys(0, 0)
         transpose_queries(0)
         load_queries(2)

@@ -17,6 +17,8 @@ AXIS = mybir.AxisListType
 P = 128
 B, LQ, LK, DIN, H = 2, 2048, 1024, 1024, 512
 FLOOR = 1e-9
+LOG_FLOOR = math.log(FLOOR)
+LN_GUARD = 2.0 ** -63
 INV_SQRT_H = 1.0 / math.sqrt(H)
 BANK = 512
 PER_BANK = BANK // P
@@ -169,12 +171,11 @@ def tile_pgwcrossattention_pa_t_kernel(
         def log_prior(u):
             z[u] = logits.tile([P, 2, LK], F32, tag="z", name="z")
             flat = z[u][:].rearrange("p i c -> p (i c)")
-            nc.vector.tensor_scalar_max(
-                out=flat, in0=plan_rows[u][:].rearrange("p i c -> p (i c)"), scalar1=FLOOR
+            nc.scalar.activation(
+                out=flat, in_=plan_rows[u][:].rearrange("p i c -> p (i c)"), func=ACT.Ln, bias=LN_GUARD
             )
             if u + PLANS_AHEAD < PAIRS:
                 load_plan(u + PLANS_AHEAD)
-            nc.scalar.activation(out=flat, in_=flat, func=ACT.Ln)
 
         def scores(u, i):
             b, c = u // PAIRS_PER_BATCH, u // 2
@@ -183,6 +184,7 @@ def tile_pgwcrossattention_pa_t_kernel(
             k_halves = keysT[b][:].bitcast(BF16).rearrange("p w (c e) -> p w c e", e=2)
             if i == 0:
                 row_max[u] = stats.tile([P, 2], F32, tag="row_max", name="row_max")
+            nc.vector.tensor_scalar_max(out=z[u][:, i, :], in0=z[u][:, i, :], scalar1=LOG_FLOOR)
             for n in range(LK // BANK):
                 bank = score_banks.tile([P, BANK], F32, tag="bank")
                 for w in range(2):

@@ -19,6 +19,7 @@ B, LQ, LK, DIN, H = 2, 2048, 1024, 1024, 512
 FLOOR = 1e-9
 LOG_FLOOR = math.log(FLOOR)
 LN_GUARD = 2.0 ** -63
+NO_CEILING = 3.0e38
 INV_SQRT_H = 1.0 / math.sqrt(H)
 BANK = 512
 PER_BANK = BANK // P
@@ -184,7 +185,14 @@ def tile_pgwcrossattention_pa_t_kernel(
             k_halves = keysT[b][:].bitcast(BF16).rearrange("p w (c e) -> p w c e", e=2)
             if i == 0:
                 row_max[u] = stats.tile([P, 2], F32, tag="row_max", name="row_max")
-            nc.vector.tensor_scalar_max(out=z[u][:, i, :], in0=z[u][:, i, :], scalar1=LOG_FLOOR)
+            nc.gpsimd.tensor_scalar(
+                out=z[u][:, i, :],
+                in0=z[u][:, i, :],
+                scalar1=NO_CEILING,
+                scalar2=LOG_FLOOR,
+                op0=ALU.min,
+                op1=ALU.max,
+            )
             for n in range(LK // BANK):
                 bank = score_banks.tile([P, BANK], F32, tag="bank")
                 for w in range(2):

@@ -36,10 +36,11 @@ CHUNK = PER_BANK
 CHUNKS = B * Q_TILES // CHUNK
 HALVES = B * GROUPS
 
-RING = 12
-LOGS_PER_ROUND = 2
-FIRST_ATTEND = RING // LOGS_PER_ROUND
+RING = 16
+LOGS_PER_ROUND = 3
+FIRST_ATTEND = 6
 MOST_ATTENDS = 2
+BY_TILE = (PAIRS - 1,)
 PLANS_AHEAD = 3
 
 FLOPS = 2 * B * (LK * DIN * H + 2 * LQ * LK * H)
@@ -74,7 +75,11 @@ def tile_pgwcrossattention_pa_t_kernel(
         ident = consts.tile([P, P], F32)
         make_identity(nc, ident[:])
         gamma_bf = consts.tile([P, 1], BF16)
+        warm = consts.tile([P, 2], F32)
+        nc.vector.memset(warm[:, 0:1], 1.0)
+        nc.scalar.activation(out=warm[:, 1:2], in_=warm[:, 0:1], func=ACT.Ln)
         gain = consts.tile([P, 1], F32)
+        exp_scale = consts.tile([P, 1], F32)
         w_codes = consts.tile([P, GROUPS, H], U32, align_bytes=64)
         bias_rows = consts.tile([P, H], BF16)
         v_codes = [
@@ -102,6 +107,7 @@ def tile_pgwcrossattention_pa_t_kernel(
         weight_banks = {}
         grouped = {}
         packed = {}
+        results = {}
 
         def load_gain():
             nc.sync.dma_start(out=gamma_bf[:], in_=gamma.partition_broadcast(P))
@@ -164,17 +170,23 @@ def tile_pgwcrossattention_pa_t_kernel(
 
         def load_plan(u):
             b, t0 = u // PAIRS_PER_BATCH, 2 * (u % PAIRS_PER_BATCH)
-            plan_rows[u] = rows.tile(
-                [P, 2, LK], BF16, tag="plan_rows", name="plan_rows", bufs=PLANS_AHEAD
-            )
-            nc.scalar.dma_start(out=plan_rows[u][:], in_=pi_view[b][:, t0 : t0 + 2, :])
+            plan_rows[u] = packs.tile([P, 2, LK], BF16, tag="weights", name="plan_rows", bufs=3)
+            if u == 0:
+                for i in range(2):
+                    nc.scalar.dma_start(out=plan_rows[u][:, i, :], in_=pi_view[b][:, t0 + i, :])
+            else:
+                nc.scalar.dma_start(out=plan_rows[u][:], in_=pi_view[b][:, t0 : t0 + 2, :])
 
         def log_prior(u):
             z[u] = logits.tile([P, 2, LK], F32, tag="z", name="z")
             flat = z[u][:].rearrange("p i c -> p (i c)")
-            nc.scalar.activation(
-                out=flat, in_=plan_rows[u][:].rearrange("p i c -> p (i c)"), func=ACT.Ln, bias=LN_GUARD
-            )
+            if u == 0:
+                for i in range(2):
+                    nc.scalar.activation(out=z[u][:, i, :], in_=plan_rows[u][:, i, :], func=ACT.Ln, bias=LN_GUARD)
+            else:
+                nc.scalar.activation(
+                    out=flat, in_=plan_rows[u][:].rearrange("p i c -> p (i c)"), func=ACT.Ln, bias=LN_GUARD
+                )
             if u + PLANS_AHEAD < PAIRS:
                 load_plan(u + PLANS_AHEAD)
 
@@ -211,62 +223,79 @@ def tile_pgwcrossattention_pa_t_kernel(
             nc.vector.tensor_reduce(
                 out=row_max[u][:, i : i + 1], in_=z[u][:, i, :], axis=AXIS.X, op=ALU.max
             )
-            if i == 1:
+            if u in BY_TILE:
+                if i == 0:
+                    shift[u] = stats.tile([P, 2], F32, tag="shift", name="shift")
+                nc.vector.tensor_scalar_mul(
+                    out=shift[u][:, i : i + 1], in0=row_max[u][:, i : i + 1], scalar1=-INV_SQRT_H
+                )
+            elif i == 1:
                 shift[u] = stats.tile([P, 2], F32, tag="shift", name="shift")
                 nc.vector.tensor_scalar_mul(
                     out=shift[u][:], in0=row_max[u][:], scalar1=-INV_SQRT_H
                 )
 
-        def exponentials(u):
-            weights[u] = packs.tile([P, 2, LK], BF16, tag="weights", name="weights", bufs=3)
-            row_sum[u] = stats.tile([P, 2], F32, tag="row_sum", name="row_sum")
-            for i in range(2):
+        def exponentials(u, tiles=(0, 1)):
+            if 0 in tiles:
+                weights[u] = packs.tile([P, 2, LK], BF16, tag="weights", name="weights", bufs=3)
+                row_sum[u] = stats.tile([P, 2], F32, tag="row_sum", name="row_sum")
+            for i in tiles:
                 nc.scalar.activation(
                     out=weights[u][:, i, :],
                     in_=z[u][:, i, :],
                     func=ACT.Exp,
                     bias=shift[u][:, i : i + 1],
-                    scale=INV_SQRT_H,
+                    scale=exp_scale[:, 0:1],
                     accum_out=row_sum[u][:, i : i + 1],
                 )
 
-        def transpose_weights(u):
+        def transpose_weights(u, tiles=(0, 1)):
             words = weights[u][:].bitcast(F32)
-            weight_banks[u] = []
-            for i in range(2):
+            for i in tiles:
                 bank = turn_banks.tile([P, BANK], F32, tag="bank")
                 for c in range(PER_BANK):
                     nc.tensor.transpose(
                         bank[:, P * c : P * (c + 1)], words[:, i, P * c : P * (c + 1)], ident[:]
                     )
-                weight_banks[u].append(bank)
+                weight_banks[(u, i)] = bank
 
-        def regroup_weights(u):
-            grouped[u] = packs.tile([P, 2, LK], BF16, tag="grouped", name="grouped", align_bytes=64)
+        def regroup_weights(u, tiles=(0, 1)):
+            if 0 in tiles:
+                grouped[u] = packs.tile(
+                    [P, 2, LK], BF16, tag="grouped", name="grouped", align_bytes=64
+                )
             words = grouped[u][:].bitcast(F32)
-            for i in range(2):
+            for i in tiles:
                 nc.scalar.copy(
                     out=words[:, i, :].rearrange("p (g c u) -> p g c u", g=GROUPS, u=2),
-                    in_=weight_banks[u][i][:].rearrange("p (g u c) -> p g c u", g=GROUPS, u=2),
+                    in_=weight_banks[(u, i)][:].rearrange("p (g u c) -> p g c u", g=GROUPS, u=2),
                 )
 
-        def quantise_weights(u):
-            codes = packs.tile([P, 2 * GROUPS * P], U32, tag="e_codes", align_bytes=64)
-            scales = packs.tile([P, 2 * GROUPS * P], U8, tag="e_scales", align_bytes=64)
+        def quantise_weights(u, tiles=(0, 1)):
+            if 0 in tiles:
+                codes = packs.tile([P, 2 * GROUPS * P], U32, tag="e_codes", align_bytes=64)
+                scales = packs.tile([P, 2 * GROUPS * P], U8, tag="e_scales", align_bytes=64)
+                packed[u] = (codes, scales)
+                inv_sum[u] = stats.tile([P, 2], F32, tag="inv_sum", name="inv_sum")
+            codes, scales = packed[u]
+            first, last = GROUPS * P * tiles[0], GROUPS * P * (tiles[-1] + 1)
             nc.vector.quantize_mx(
-                out=codes[:].bitcast(FP8X4),
-                scales=scales[:],
-                in_=grouped[u][:].rearrange("p i c -> p (i c)"),
+                out=codes[:, first:last].bitcast(FP8X4),
+                scales=scales[:, first:last],
+                in_=grouped[u][:, tiles[0] : tiles[-1] + 1, :].rearrange("p i c -> p (i c)"),
             )
-            packed[u] = (codes, scales)
-            inv_sum[u] = stats.tile([P, 2], F32, tag="inv_sum", name="inv_sum")
-            nc.vector.reciprocal(out=inv_sum[u][:], in_=row_sum[u][:])
+            nc.vector.reciprocal(
+                out=inv_sum[u][:, tiles[0] : tiles[-1] + 1], in_=row_sum[u][:, tiles[0] : tiles[-1] + 1]
+            )
 
-        def weighted_sums(u):
+        def weighted_sums(u, tiles=(0, 1)):
             b, t0 = u // PAIRS_PER_BATCH, 2 * (u % PAIRS_PER_BATCH)
             codes, scales = packed[u]
-            sums = []
-            for i in range(2):
+            if 0 in tiles:
+                results[u] = packs.tile([P, 2, H], F32, tag="result", name="result")
+            result = results[u]
+            sums = {}
+            for i in tiles:
                 bank = sum_banks.tile([P, BANK], F32, tag="bank")
                 for g in range(GROUPS):
                     cols = slice(P * (GROUPS * i + g), P * (GROUPS * i + g + 1))
@@ -279,54 +308,66 @@ def tile_pgwcrossattention_pa_t_kernel(
                         start=(g == 0),
                         stop=(g == GROUPS - 1),
                     )
-                sums.append(bank)
-            result = packs.tile([P, 2, H], F32, tag="result")
-            nc.vector.tensor_scalar(
-                out=result[:, 0, :],
-                in0=sums[0][:],
-                scalar1=inv_sum[u][:, 0:1],
-                scalar2=None,
-                op0=ALU.mult,
+                sums[i] = bank
+            for i in tiles:
+                if i == 0:
+                    nc.vector.tensor_scalar(
+                        out=result[:, i, :],
+                        in0=sums[i][:],
+                        scalar1=inv_sum[u][:, i : i + 1],
+                        scalar2=None,
+                        op0=ALU.mult,
+                    )
+                else:
+                    nc.scalar.activation(
+                        out=result[:, i, :],
+                        in_=sums[i][:],
+                        func=ACT.Copy,
+                        scale=inv_sum[u][:, i : i + 1],
+                    )
+            nc.sync.dma_start(
+                out=out_view[b][:, t0 + tiles[0] : t0 + tiles[-1] + 1, :],
+                in_=result[:, tiles[0] : tiles[-1] + 1, :],
             )
-            nc.scalar.activation(
-                out=result[:, 1, :], in_=sums[1][:], func=ACT.Copy, scale=inv_sum[u][:, 1:2]
-            )
-            nc.sync.dma_start(out=out_view[b][:, t0 : t0 + 2, :], in_=result[:])
 
         def load_values(n):
             b, g = n // GROUPS, n % GROUPS
-            value_rows[n] = rows.tile([P, PER_BANK, DIN], BF16, tag="value_rows", name="value_rows")
-            nc.sync.dma_start(
-                out=value_rows[n][:].rearrange("p (u i) d -> p u (i d)", u=2), in_=v_view[b][g]
-            )
+            for u in range(2):
+                value_rows[(n, u)] = packs.tile([P, 2, DIN], BF16, tag="result", name="value_rows")
+                nc.sync.dma_start(
+                    out=value_rows[(n, u)][:].rearrange("p i d -> p (i d)"), in_=v_view[b][g][:, u, :]
+                )
 
         def quantise_values_in(n):
-            words = value_rows[n][:].bitcast(F32)
-            lined = packs.tile(
-                [P, GROUPS, 4 * BANK], BF16, tag="v_in_grouped", bufs=1, align_bytes=64
-            )
-            lined_words = lined[:].bitcast(F32).rearrange("p d (c u) -> p d c u", u=2)
-            for t in range(PER_BANK):
-                bank = turn_banks.tile([P, BANK], F32, tag="bank")
-                for d in range(GROUPS):
-                    for u in range(2):
-                        col = P * (2 * d + u)
-                        nc.tensor.transpose(
-                            bank[:, col : col + P],
-                            words[:, t, PASS_WORDS * d + u : PASS_WORDS * (d + 1) : 2],
-                            ident[:],
-                        )
-                nc.scalar.copy(
-                    out=lined_words[:, :, P * t : P * (t + 1), :],
-                    in_=bank[:].rearrange("p (d u c) -> p d c u", d=GROUPS, u=2),
-                )
             codes = packs.tile([P, GROUPS, BANK], U32, tag="v_in_codes", bufs=1, align_bytes=64)
             scales = packs.tile([P, GROUPS, BANK], U8, tag="v_in_scales", bufs=1, align_bytes=64)
-            nc.vector.quantize_mx(
-                out=codes[:].rearrange("p d c -> p (d c)").bitcast(FP8X4),
-                scales=scales[:].rearrange("p d c -> p (d c)"),
-                in_=lined[:].rearrange("p d c -> p (d c)"),
-            )
+            lined = []
+            for d in range(GROUPS):
+                lined.append(
+                    packs.tile([P, 4 * BANK], BF16, tag="grouped", name="lined", align_bytes=64)
+                )
+            for u in range(2):
+                words = value_rows[(n, u)][:].bitcast(F32)
+                for d in range(GROUPS):
+                    bank = turn_banks.tile([P, BANK], F32, tag="bank")
+                    for i in range(2):
+                        for e in range(2):
+                            col = P * (2 * i + e)
+                            nc.tensor.transpose(
+                                bank[:, col : col + P],
+                                words[:, i, PASS_WORDS * d + e : PASS_WORDS * (d + 1) : 2],
+                                ident[:],
+                            )
+                    nc.scalar.copy(
+                        out=lined[d][:].bitcast(F32)[:, BANK * u : BANK * (u + 1)].rearrange(
+                            "p (i c e) -> p i c e", i=2, e=2
+                        ),
+                        in_=bank[:].rearrange("p (i e c) -> p i c e", i=2, e=2),
+                    )
+            for d in range(GROUPS):
+                nc.vector.quantize_mx(
+                    out=codes[:, d, :].bitcast(FP8X4), scales=scales[:, d, :], in_=lined[d][:]
+                )
             value_in[n] = (codes, scales)
 
         def project_values(n):
@@ -391,14 +432,17 @@ def tile_pgwcrossattention_pa_t_kernel(
         x = 0
         logged = 0
         for r in range(PAIRS):
-            if logged < RING:
-                for u in range(logged, logged + LOGS_PER_ROUND):
-                    log_prior(u)
-                logged += LOGS_PER_ROUND
-            elif logged < PAIRS and x >= PAIRS - RING:
-                for u in range(logged, PAIRS):
-                    log_prior(u)
-                logged = PAIRS
+            for u in range(logged, min(PAIRS, logged + LOGS_PER_ROUND)):
+                log_prior(u)
+                if u == PAIRS - 1:
+                    nc.scalar.activation(
+                        out=exp_scale[:],
+                        in_=z[u][:, 1, LK - 1 : LK],
+                        func=ACT.Copy,
+                        scale=0.0,
+                        bias=INV_SQRT_H,
+                    )
+            logged = min(PAIRS, logged + LOGS_PER_ROUND)
             attends = 0 if r < FIRST_ATTEND else min(MOST_ATTENDS, r - x)
             if attends > 0:
                 attend_front(x)
@@ -406,9 +450,13 @@ def tile_pgwcrossattention_pa_t_kernel(
             if attends > 0:
                 attend_back(x)
                 x += 1
+            if r in BY_TILE:
+                exponentials(r, (0,))
             if attends > 1:
                 attend_front(x)
             scores(r, 1)
+            if r in BY_TILE:
+                exponentials(r, (1,))
             if attends > 1:
                 attend_back(x)
                 x += 1
@@ -427,7 +475,16 @@ def tile_pgwcrossattention_pa_t_kernel(
                     load_queries(c + 2)
             if PAIRS_PER_BATCH - 2 <= r < PAIRS_PER_BATCH:
                 transpose_keys(1, r - (PAIRS_PER_BATCH - 2))
-        while x < PAIRS + 2:
-            attend_front(x)
-            attend_back(x)
-            x += 1
+        last = PAIRS - 1
+        quantise_weights(last - 2)
+        transpose_weights(last - 1)
+        regroup_weights(last - 1)
+        weighted_sums(last - 2)
+        for i in range(2):
+            transpose_weights(last, (i,))
+            regroup_weights(last, (i,))
+        quantise_weights(last - 1)
+        weighted_sums(last - 1)
+        for i in range(2):
+            quantise_weights(last, (i,))
+            weighted_sums(last, (i,))

@@ -57,9 +57,9 @@ def tile_pgwcrossattention_pa_t_kernel(
         logits = ctx.enter_context(tc.tile_pool(name="logits", bufs=RING))
         packs = ctx.enter_context(tc.tile_pool(name="packs", bufs=2))
         stats = ctx.enter_context(tc.tile_pool(name="stats", bufs=FIRST_ATTEND + 2))
-        score_banks = ctx.enter_context(tc.psum_pool(name="score_banks", bufs=4))
-        turn_banks = ctx.enter_context(tc.psum_pool(name="turn_banks", bufs=2))
-        sum_banks = ctx.enter_context(tc.psum_pool(name="sum_banks", bufs=2))
+        score_banks = ctx.enter_context(tc.psum_pool(name="score_banks", bufs=8))
+        turn_banks = score_banks
+        sum_banks = score_banks
 
         q_view = [q[b].rearrange("(p t) h -> p t h", t=Q_TILES) for b in range(B)]
         pi_view = [pi_star[b].rearrange("(p t) c -> p t c", t=Q_TILES) for b in range(B)]

@@ -41,6 +41,7 @@ LOGS_PER_ROUND = 3
 FIRST_ATTEND = 6
 MOST_ATTENDS = 2
 BY_TILE = (PAIRS - 1,)
+KEYS_AT = 4
 PLANS_AHEAD = 3
 
 FLOPS = 2 * B * (LK * DIN * H + 2 * LQ * LK * H)
@@ -108,6 +109,27 @@ def tile_pgwcrossattention_pa_t_kernel(
         grouped = {}
         packed = {}
         results = {}
+        value_lined = {}
+        open_banks = {}
+        waiting = []
+        written = [0]
+
+        def queue_bank(key, sources, then, args):
+            for slot in range(PER_BANK):
+                waiting.append((key, slot, sources[slot], then if slot == PER_BANK - 1 else None, args))
+
+        def write_waiting(places):
+            left = len(waiting) - written[0]
+            for k in range((left + places - 1) // places):
+                key, slot, source, then, args = waiting[written[0]]
+                written[0] += 1
+                if slot == 0:
+                    open_banks[key] = turn_banks.tile([P, BANK], F32, tag="bank", name="bank")
+                nc.tensor.transpose(
+                    open_banks[key][:, P * slot : P * (slot + 1)], source, ident[:]
+                )
+                if then is not None:
+                    then(*args)
 
         def load_gain():
             nc.sync.dma_start(out=gamma_bf[:], in_=gamma.partition_broadcast(P))
@@ -132,21 +154,22 @@ def tile_pgwcrossattention_pa_t_kernel(
             tiles = slice(PER_BANK * half, PER_BANK * (half + 1))
             nc.sync.dma_start(out=key_rows[b][:, tiles, :], in_=k_view[b][:, tiles, :])
 
-        def transpose_keys(b, half):
-            if half == 0:
+        def queue_keys(b, half, w):
+            if half == 0 and w == 0:
                 keysT[b] = turned.tile([P, 2, LK], F32, tag="keysT", name="keysT")
             words = key_rows[b][:].bitcast(F32)
-            for w in range(2):
-                bank = turn_banks.tile([P, BANK], F32, tag="bank")
-                for i in range(PER_BANK):
-                    nc.tensor.transpose(
-                        bank[:, P * i : P * (i + 1)],
-                        words[:, PER_BANK * half + i, P * w : P * (w + 1)],
-                        ident[:],
-                    )
-                nc.vector.tensor_copy(
-                    out=keysT[b][:, w, BANK * half : BANK * (half + 1)], in_=bank[:]
-                )
+            queue_bank(
+                ("k", b, half, w),
+                [words[:, PER_BANK * half + i, P * w : P * (w + 1)] for i in range(PER_BANK)],
+                keep_keys,
+                (b, half, w),
+            )
+
+        def keep_keys(b, half, w):
+            nc.vector.tensor_copy(
+                out=keysT[b][:, w, BANK * half : BANK * (half + 1)],
+                in_=open_banks[("k", b, half, w)][:],
+            )
 
         def load_queries(c):
             b, t0 = c // (CHUNKS // B), CHUNK * (c % (CHUNKS // B))
@@ -155,18 +178,19 @@ def tile_pgwcrossattention_pa_t_kernel(
             )
             nc.sync.dma_start(out=query_rows[c][:], in_=q_view[b][:, t0 : t0 + CHUNK, :])
 
-        def transpose_queries(c):
-            queriesT[c] = turned.tile([P, 2, CHUNK * P], F32, tag="queriesT", name="queriesT")
+        def queue_queries(c, w):
+            if w == 0:
+                queriesT[c] = turned.tile([P, 2, CHUNK * P], F32, tag="queriesT", name="queriesT")
             words = query_rows[c][:].bitcast(F32)
-            for w in range(2):
-                bank = turn_banks.tile([P, BANK], F32, tag="bank")
-                for j in range(CHUNK):
-                    nc.tensor.transpose(
-                        bank[:, P * j : P * (j + 1)],
-                        words[:, j, P * w : P * (w + 1)],
-                        ident[:],
-                    )
-                nc.scalar.copy(out=queriesT[c][:, w, :], in_=bank[:])
+            queue_bank(
+                ("q", c, w),
+                [words[:, j, P * w : P * (w + 1)] for j in range(CHUNK)],
+                keep_queries,
+                (c, w),
+            )
+
+        def keep_queries(c, w):
+            nc.scalar.copy(out=queriesT[c][:, w, :], in_=open_banks[("q", c, w)][:])
 
         def load_plan(u):
             b, t0 = u // PAIRS_PER_BATCH, 2 * (u % PAIRS_PER_BATCH)
@@ -205,6 +229,7 @@ def tile_pgwcrossattention_pa_t_kernel(
                 op0=ALU.min,
                 op1=ALU.max,
             )
+            places = 4 * (LK // BANK) - 1
             for n in range(LK // BANK):
                 bank = score_banks.tile([P, BANK], F32, tag="bank")
                 for w in range(2):
@@ -216,6 +241,9 @@ def tile_pgwcrossattention_pa_t_kernel(
                             start=(w == 0 and e == 0),
                             stop=(w == 1 and e == 1),
                         )
+                        if places > 0:
+                            write_waiting(places)
+                            places -= 1
                 cols = z[u][:, i, BANK * n : BANK * (n + 1)]
                 nc.vector.scalar_tensor_tensor(
                     out=cols, in0=cols, scalar=gain[:, 0:1], in1=bank[:], op0=ALU.mult, op1=ALU.add
@@ -249,27 +277,24 @@ def tile_pgwcrossattention_pa_t_kernel(
                     accum_out=row_sum[u][:, i : i + 1],
                 )
 
-        def transpose_weights(u, tiles=(0, 1)):
+        def queue_weights(u, i):
             words = weights[u][:].bitcast(F32)
-            for i in tiles:
-                bank = turn_banks.tile([P, BANK], F32, tag="bank")
-                for c in range(PER_BANK):
-                    nc.tensor.transpose(
-                        bank[:, P * c : P * (c + 1)], words[:, i, P * c : P * (c + 1)], ident[:]
-                    )
-                weight_banks[(u, i)] = bank
+            queue_bank(
+                ("e", u, i),
+                [words[:, i, P * c : P * (c + 1)] for c in range(PER_BANK)],
+                regroup_weights,
+                (u, i),
+            )
 
-        def regroup_weights(u, tiles=(0, 1)):
-            if 0 in tiles:
+        def regroup_weights(u, i):
+            if i == 0:
                 grouped[u] = packs.tile(
                     [P, 2, LK], BF16, tag="grouped", name="grouped", align_bytes=64
                 )
-            words = grouped[u][:].bitcast(F32)
-            for i in tiles:
-                nc.scalar.copy(
-                    out=words[:, i, :].rearrange("p (g c u) -> p g c u", g=GROUPS, u=2),
-                    in_=weight_banks[(u, i)][:].rearrange("p (g u c) -> p g c u", g=GROUPS, u=2),
-                )
+            nc.scalar.copy(
+                out=grouped[u][:].bitcast(F32)[:, i, :].rearrange("p (g c u) -> p g c u", g=GROUPS, u=2),
+                in_=open_banks[("e", u, i)][:].rearrange("p (g u c) -> p g c u", g=GROUPS, u=2),
+            )
 
         def quantise_weights(u, tiles=(0, 1)):
             if 0 in tiles:
@@ -338,35 +363,40 @@ def tile_pgwcrossattention_pa_t_kernel(
                     out=value_rows[(n, u)][:].rearrange("p i d -> p (i d)"), in_=v_view[b][g][:, u, :]
                 )
 
+        def queue_values(n, u):
+            if u == 0:
+                value_lined[n] = []
+                for d in range(GROUPS):
+                    value_lined[n].append(
+                        packs.tile([P, 4 * BANK], BF16, tag="grouped", name="lined", align_bytes=64)
+                    )
+            words = value_rows[(n, u)][:].bitcast(F32)
+            for d in range(GROUPS):
+                queue_bank(
+                    ("v", n, u, d),
+                    [
+                        words[:, i, PASS_WORDS * d + e : PASS_WORDS * (d + 1) : 2]
+                        for i in range(2)
+                        for e in range(2)
+                    ],
+                    keep_values,
+                    (n, u, d),
+                )
+
+        def keep_values(n, u, d):
+            nc.scalar.copy(
+                out=value_lined[n][d][:].bitcast(F32)[:, BANK * u : BANK * (u + 1)].rearrange(
+                    "p (i c e) -> p i c e", i=2, e=2
+                ),
+                in_=open_banks[("v", n, u, d)][:].rearrange("p (i e c) -> p i c e", i=2, e=2),
+            )
+
         def quantise_values_in(n):
             codes = packs.tile([P, GROUPS, BANK], U32, tag="v_in_codes", bufs=1, align_bytes=64)
             scales = packs.tile([P, GROUPS, BANK], U8, tag="v_in_scales", bufs=1, align_bytes=64)
-            lined = []
-            for d in range(GROUPS):
-                lined.append(
-                    packs.tile([P, 4 * BANK], BF16, tag="grouped", name="lined", align_bytes=64)
-                )
-            for u in range(2):
-                words = value_rows[(n, u)][:].bitcast(F32)
-                for d in range(GROUPS):
-                    bank = turn_banks.tile([P, BANK], F32, tag="bank")
-                    for i in range(2):
-                        for e in range(2):
-                            col = P * (2 * i + e)
-                            nc.tensor.transpose(
-                                bank[:, col : col + P],
-                                words[:, i, PASS_WORDS * d + e : PASS_WORDS * (d + 1) : 2],
-                                ident[:],
-                            )
-                    nc.scalar.copy(
-                        out=lined[d][:].bitcast(F32)[:, BANK * u : BANK * (u + 1)].rearrange(
-                            "p (i c e) -> p i c e", i=2, e=2
-                        ),
-                        in_=bank[:].rearrange("p (i e c) -> p i c e", i=2, e=2),
-                    )
             for d in range(GROUPS):
                 nc.vector.quantize_mx(
-                    out=codes[:, d, :].bitcast(FP8X4), scales=scales[:, d, :], in_=lined[d][:]
+                    out=codes[:, d, :].bitcast(FP8X4), scales=scales[:, d, :], in_=value_lined[n][d][:]
                 )
             value_in[n] = (codes, scales)
 
@@ -403,11 +433,10 @@ def tile_pgwcrossattention_pa_t_kernel(
             if 0 <= x - 2 < PAIRS:
                 quantise_weights(x - 2)
             if 0 <= x - 1 < PAIRS:
-                transpose_weights(x - 1)
+                queue_weights(x - 1, 0)
+                queue_weights(x - 1, 1)
             if x < PAIRS:
                 exponentials(x)
-            if 0 <= x - 1 < PAIRS:
-                regroup_weights(x - 1)
 
         def attend_back(x):
             if 0 <= x - 2 < PAIRS:
@@ -422,12 +451,25 @@ def tile_pgwcrossattention_pa_t_kernel(
         load_queries(1)
         load_values(0)
         load_weight()
-        transpose_keys(0, 0)
-        transpose_queries(0)
+        for w in range(2):
+            queue_keys(0, 0, w)
+        for w in range(2):
+            queue_queries(0, w)
+        write_waiting(1)
         load_queries(2)
-        transpose_keys(0, 1)
+        for w in range(2):
+            queue_keys(0, 1, w)
+        write_waiting(1)
         load_keys(1, 0)
         load_keys(1, 1)
+
+        def queue_beside(r, i):
+            if r < 2 * HALVES and r % 2 == 0:
+                queue_values(r // 2, i)
+            if r % 2 == 1 and (r + 1) // 2 < CHUNKS:
+                queue_queries((r + 1) // 2, i)
+            if KEYS_AT <= r < KEYS_AT + 2:
+                queue_keys(1, r - KEYS_AT, i)
 
         x = 0
         logged = 0
@@ -446,6 +488,7 @@ def tile_pgwcrossattention_pa_t_kernel(
             attends = 0 if r < FIRST_ATTEND else min(MOST_ATTENDS, r - x)
             if attends > 0:
                 attend_front(x)
+            queue_beside(r, 0)
             scores(r, 0)
             if attends > 0:
                 attend_back(x)
@@ -454,6 +497,7 @@ def tile_pgwcrossattention_pa_t_kernel(
                 exponentials(r, (0,))
             if attends > 1:
                 attend_front(x)
+            queue_beside(r, 1)
             scores(r, 1)
             if r in BY_TILE:
                 exponentials(r, (1,))
@@ -468,21 +512,17 @@ def tile_pgwcrossattention_pa_t_kernel(
                         load_values(n + 1)
                 else:
                     project_values(n)
-            c = (r + 1) // 2
-            if r % 2 == 1 and c < CHUNKS:
-                transpose_queries(c)
-                if c + 2 < CHUNKS:
-                    load_queries(c + 2)
-            if PAIRS_PER_BATCH - 2 <= r < PAIRS_PER_BATCH:
-                transpose_keys(1, r - (PAIRS_PER_BATCH - 2))
+            if r % 2 == 1 and (r + 1) // 2 + 2 < CHUNKS:
+                load_queries((r + 1) // 2 + 2)
         last = PAIRS - 1
         quantise_weights(last - 2)
-        transpose_weights(last - 1)
-        regroup_weights(last - 1)
-        weighted_sums(last - 2)
-        for i in range(2):
-            transpose_weights(last, (i,))
-            regroup_weights(last, (i,))
+        for u in (last - 1, last):
+            for i in range(2):
+                queue_weights(u, i)
+            if u == last - 1:
+                write_waiting(1)
+                weighted_sums(last - 2)
+        write_waiting(1)
         quantise_weights(last - 1)
         weighted_sums(last - 1)
         for i in range(2):

@@ -42,6 +42,7 @@ FIRST_ATTEND = 6
 MOST_ATTENDS = 2
 BY_TILE = (PAIRS - 1,)
 KEYS_AT = 4
+FLOOR_PIECE = 512
 PLANS_AHEAD = 3
 
 FLOPS = 2 * B * (LK * DIN * H + 2 * LQ * LK * H)
@@ -221,14 +222,11 @@ def tile_pgwcrossattention_pa_t_kernel(
             k_halves = keysT[b][:].bitcast(BF16).rearrange("p w (c e) -> p w c e", e=2)
             if i == 0:
                 row_max[u] = stats.tile([P, 2], F32, tag="row_max", name="row_max")
-            nc.gpsimd.tensor_scalar(
-                out=z[u][:, i, :],
-                in0=z[u][:, i, :],
-                scalar1=NO_CEILING,
-                scalar2=LOG_FLOOR,
-                op0=ALU.min,
-                op1=ALU.max,
-            )
+            for part in range(LK // FLOOR_PIECE):
+                cut = z[u][:, i, FLOOR_PIECE * part : FLOOR_PIECE * (part + 1)]
+                nc.gpsimd.tensor_scalar(
+                    out=cut, in0=cut, scalar1=NO_CEILING, scalar2=LOG_FLOOR, op0=ALU.min, op1=ALU.max
+                )
             places = 4 * (LK // BANK) - 1
             for n in range(LK // BANK):
                 bank = score_banks.tile([P, BANK], F32, tag="bank")

import math
from contextlib import ExitStack

import concourse.mybir as mybir
from concourse.masks import make_identity

F32 = mybir.dt.float32
BF16 = mybir.dt.bfloat16
I32 = mybir.dt.int32
U32 = mybir.dt.uint32
U8 = mybir.dt.uint8
FP8X4 = mybir.dt.float8_e4m3fn_x4
ALU = mybir.AluOpType
ACT = mybir.ActivationFunctionType
AXIS = mybir.AxisListType

P = 128
B, LQ, LK, DIN, H = 2, 2048, 1024, 1024, 512
FLOOR = 1e-9
LOG_FLOOR = math.log(FLOOR)
LN_GUARD = 2.0 ** -63
NO_CEILING = 3.0e38
INV_SQRT_H = 1.0 / math.sqrt(H)
BANK = 512
PER_BANK = BANK // P
QUADRANT = 32
K_PASS = 4 * P
PASS_WORDS = K_PASS // 2
GROUPS = LK // K_PASS

Q_TILES = LQ // P
KEY_TILES = LK // P
PAIRS_PER_BATCH = Q_TILES // 2
PAIRS = B * PAIRS_PER_BATCH
CHUNK = PER_BANK
CHUNKS = B * Q_TILES // CHUNK
HALVES = B * GROUPS

RING = 16
LOGS_PER_ROUND = 3
FIRST_ATTEND = 6
MOST_ATTENDS = 2
BY_TILE = (PAIRS - 1,)
KEYS_AT = 4
FLOOR_PIECE = 512
PLANS_AHEAD = 3

FLOPS = 2 * B * (LK * DIN * H + 2 * LQ * LK * H)


def tile_pgwcrossattention_pa_t_kernel(
    tc, q, k, v_ret, pi_star, Wv_words, Wv_scales, bv, gamma, out
):
    nc = tc.nc
    with ExitStack() as ctx:
        consts = ctx.enter_context(tc.tile_pool(name="consts", bufs=1))
        rows = ctx.enter_context(tc.tile_pool(name="rows", bufs=1))
        turned = ctx.enter_context(tc.tile_pool(name="turned", bufs=2))
        logits = ctx.enter_context(tc.tile_pool(name="logits", bufs=RING))
        packs = ctx.enter_context(tc.tile_pool(name="packs", bufs=2))
        stats = ctx.enter_context(tc.tile_pool(name="stats", bufs=FIRST_ATTEND + 2))
        score_banks = ctx.enter_context(tc.psum_pool(name="score_banks", bufs=8))
        turn_banks = score_banks
        sum_banks = score_banks

        q_view = [q[b].rearrange("(p t) h -> p t h", t=Q_TILES) for b in range(B)]
        pi_view = [pi_star[b].rearrange("(p t) c -> p t c", t=Q_TILES) for b in range(B)]
        out_view = [out[b].rearrange("(p t) h -> p t h", t=Q_TILES) for b in range(B)]
        k_view = [k[b].rearrange("(t p) h -> p t h", p=P) for b in range(B)]
        v_view = [
            v_ret[b].rearrange("(g u p i) d -> g p u (i d)", g=GROUPS, u=2, p=P, i=2)
            for b in range(B)
        ]

        w_scales = consts.tile([P, GROUPS, H], U8, align_bytes=64)
        nc.vector.memset(w_scales[:].rearrange("p d n -> p (d n)").bitcast(I32), 0)
        ident = consts.tile([P, P], F32)
        make_identity(nc, ident[:])
        gamma_bf = consts.tile([P, 1], BF16)
        warm = consts.tile([P, 2], F32)
        nc.vector.memset(warm[:, 0:1], 1.0)
        nc.scalar.activation(out=warm[:, 1:2], in_=warm[:, 0:1], func=ACT.Ln)
        gain = consts.tile([P, 1], F32)
        exp_scale = consts.tile([P, 1], F32)
        w_codes = consts.tile([P, GROUPS, H], U32, align_bytes=64)
        bias_rows = consts.tile([P, H], BF16)
        v_codes = [
            consts.tile([P, GROUPS, H], U32, name="v_codes%d" % b, align_bytes=64)
            for b in range(B)
        ]
        v_scales = [
            consts.tile([P, GROUPS, H], U8, name="v_scales%d" % b, align_bytes=64)
            for b in range(B)
        ]

        key_rows = {}
        keysT = {}
        query_rows = {}
        queriesT = {}
        plan_rows = {}
        value_rows = {}
        value_in = {}
        z = {}
        row_max = {}
        shift = {}
        row_sum = {}
        inv_sum = {}
        weights = {}
        weight_banks = {}
        grouped = {}
        packed = {}
        results = {}
        value_lined = {}
        open_banks = {}
        waiting = []
        written = [0]

        def queue_bank(key, sources, then, args):
            for slot in range(PER_BANK):
                waiting.append((key, slot, sources[slot], then if slot == PER_BANK - 1 else None, args))

        def write_waiting(places):
            left = len(waiting) - written[0]
            for k in range((left + places - 1) // places):
                key, slot, source, then, args = waiting[written[0]]
                written[0] += 1
                if slot == 0:
                    open_banks[key] = turn_banks.tile([P, BANK], F32, tag="bank", name="bank")
                nc.tensor.transpose(
                    open_banks[key][:, P * slot : P * (slot + 1)], source, ident[:]
                )
                if then is not None:
                    then(*args)

        def load_gain():
            nc.sync.dma_start(out=gamma_bf[:], in_=gamma.partition_broadcast(P))
            nc.vector.tensor_scalar_mul(out=gain[:], in0=gamma_bf[:], scalar1=math.sqrt(H))

        def load_weight():
            for d in range(GROUPS):
                nc.sync.dma_start(
                    out=w_codes[:, d, :].bitcast(I32),
                    in_=Wv_words[d].rearrange("p n t -> p (n t)").bitcast(I32),
                )
            for quad in range(P // QUADRANT):
                nc.sync.dma_start(
                    out=w_scales[QUADRANT * quad : QUADRANT * quad + 4, :, :].bitcast(I32),
                    in_=Wv_scales[:, 4 * quad : 4 * quad + 4, :].rearrange("d r n -> r d n").bitcast(I32),
                )
            nc.sync.dma_start(out=bias_rows[:], in_=bv.partition_broadcast(P))

        def load_keys(b, half):
            if half == 0:
                key_rows[b] = rows.tile([P, KEY_TILES, H], BF16, tag="key_rows", name="key_rows")
            tiles = slice(PER_BANK * half, PER_BANK * (half + 1))
            nc.sync.dma_start(out=key_rows[b][:, tiles, :], in_=k_view[b][:, tiles, :])

        def queue_keys(b, half, w):
            if half == 0 and w == 0:
                keysT[b] = turned.tile([P, 2, LK], F32, tag="keysT", name="keysT")
            words = key_rows[b][:].bitcast(F32)
            queue_bank(
                ("k", b, half, w),
                [words[:, PER_BANK * half + i, P * w : P * (w + 1)] for i in range(PER_BANK)],
                keep_keys,
                (b, half, w),
            )

        def keep_keys(b, half, w):
            nc.vector.tensor_copy(
                out=keysT[b][:, w, BANK * half : BANK * (half + 1)],
                in_=open_banks[("k", b, half, w)][:],
            )

        def load_queries(c):
            b, t0 = c // (CHUNKS // B), CHUNK * (c % (CHUNKS // B))
            query_rows[c] = rows.tile(
                [P, CHUNK, H], BF16, tag="query_rows", name="query_rows", bufs=2
            )
            nc.sync.dma_start(out=query_rows[c][:], in_=q_view[b][:, t0 : t0 + CHUNK, :])

        def queue_queries(c, w):
            if w == 0:
                queriesT[c] = turned.tile([P, 2, CHUNK * P], F32, tag="queriesT", name="queriesT")
            words = query_rows[c][:].bitcast(F32)
            queue_bank(
                ("q", c, w),
                [words[:, j, P * w : P * (w + 1)] for j in range(CHUNK)],
                keep_queries,
                (c, w),
            )

        def keep_queries(c, w):
            nc.scalar.copy(out=queriesT[c][:, w, :], in_=open_banks[("q", c, w)][:])

        def load_plan(u):
            b, t0 = u // PAIRS_PER_BATCH, 2 * (u % PAIRS_PER_BATCH)
            plan_rows[u] = packs.tile([P, 2, LK], BF16, tag="weights", name="plan_rows", bufs=3)
            if u == 0:
                for i in range(2):
                    nc.scalar.dma_start(out=plan_rows[u][:, i, :], in_=pi_view[b][:, t0 + i, :])
            else:
                nc.scalar.dma_start(out=plan_rows[u][:], in_=pi_view[b][:, t0 : t0 + 2, :])

        def log_prior(u):
            z[u] = logits.tile([P, 2, LK], F32, tag="z", name="z")
            flat = z[u][:].rearrange("p i c -> p (i c)")
            if u == 0:
                for i in range(2):
                    nc.scalar.activation(out=z[u][:, i, :], in_=plan_rows[u][:, i, :], func=ACT.Ln, bias=LN_GUARD)
            else:
                nc.scalar.activation(
                    out=flat, in_=plan_rows[u][:].rearrange("p i c -> p (i c)"), func=ACT.Ln, bias=LN_GUARD
                )
            if u + PLANS_AHEAD < PAIRS:
                load_plan(u + PLANS_AHEAD)

        def scores(u, i):
            b, c = u // PAIRS_PER_BATCH, u // 2
            j = 2 * (u % 2) + i
            q_halves = queriesT[c][:].bitcast(BF16).rearrange("p w (c e) -> p w c e", e=2)
            k_halves = keysT[b][:].bitcast(BF16).rearrange("p w (c e) -> p w c e", e=2)
            if i == 0:
                row_max[u] = stats.tile([P, 2], F32, tag="row_max", name="row_max")
            for part in range(LK // FLOOR_PIECE):
                cut = z[u][:, i, FLOOR_PIECE * part : FLOOR_PIECE * (part + 1)]
                nc.gpsimd.tensor_scalar(
                    out=cut, in0=cut, scalar1=NO_CEILING, scalar2=LOG_FLOOR, op0=ALU.min, op1=ALU.max
                )
            places = 4 * (LK // BANK) - 1
            for n in range(LK // BANK):
                bank = score_banks.tile([P, BANK], F32, tag="bank")
                for w in range(2):
                    for e in range(2):
                        nc.tensor.matmul(
                            out=bank[:],
                            lhsT=q_halves[:, w, P * j : P * (j + 1), e],
                            rhs=k_halves[:, w, BANK * n : BANK * (n + 1), e],
                            start=(w == 0 and e == 0),
                            stop=(w == 1 and e == 1),
                        )
                        if places > 0:
                            write_waiting(places)
                            places -= 1
                cols = z[u][:, i, BANK * n : BANK * (n + 1)]
                nc.vector.scalar_tensor_tensor(
                    out=cols, in0=cols, scalar=gain[:, 0:1], in1=bank[:], op0=ALU.mult, op1=ALU.add
                )
            nc.vector.tensor_reduce(
                out=row_max[u][:, i : i + 1], in_=z[u][:, i, :], axis=AXIS.X, op=ALU.max
            )
            if u in BY_TILE:
                if i == 0:
                    shift[u] = stats.tile([P, 2], F32, tag="shift", name="shift")
                nc.vector.tensor_scalar_mul(
                    out=shift[u][:, i : i + 1], in0=row_max[u][:, i : i + 1], scalar1=-INV_SQRT_H
                )
            elif i == 1:
                shift[u] = stats.tile([P, 2], F32, tag="shift", name="shift")
                nc.vector.tensor_scalar_mul(
                    out=shift[u][:], in0=row_max[u][:], scalar1=-INV_SQRT_H
                )

        def exponentials(u, tiles=(0, 1)):
            if 0 in tiles:
                weights[u] = packs.tile([P, 2, LK], BF16, tag="weights", name="weights", bufs=3)
                row_sum[u] = stats.tile([P, 2], F32, tag="row_sum", name="row_sum")
            for i in tiles:
                nc.scalar.activation(
                    out=weights[u][:, i, :],
                    in_=z[u][:, i, :],
                    func=ACT.Exp,
                    bias=shift[u][:, i : i + 1],
                    scale=exp_scale[:, 0:1],
                    accum_out=row_sum[u][:, i : i + 1],
                )

        def queue_weights(u, i):
            words = weights[u][:].bitcast(F32)
            queue_bank(
                ("e", u, i),
                [words[:, i, P * c : P * (c + 1)] for c in range(PER_BANK)],
                regroup_weights,
                (u, i),
            )

        def regroup_weights(u, i):
            if i == 0:
                grouped[u] = packs.tile(
                    [P, 2, LK], BF16, tag="grouped", name="grouped", align_bytes=64
                )
            nc.scalar.copy(
                out=grouped[u][:].bitcast(F32)[:, i, :].rearrange("p (g c u) -> p g c u", g=GROUPS, u=2),
                in_=open_banks[("e", u, i)][:].rearrange("p (g u c) -> p g c u", g=GROUPS, u=2),
            )

        def quantise_weights(u, tiles=(0, 1)):
            if 0 in tiles:
                codes = packs.tile([P, 2 * GROUPS * P], U32, tag="e_codes", align_bytes=64)
                scales = packs.tile([P, 2 * GROUPS * P], U8, tag="e_scales", align_bytes=64)
                packed[u] = (codes, scales)
                inv_sum[u] = stats.tile([P, 2], F32, tag="inv_sum", name="inv_sum")
            codes, scales = packed[u]
            first, last = GROUPS * P * tiles[0], GROUPS * P * (tiles[-1] + 1)
            nc.vector.quantize_mx(
                out=codes[:, first:last].bitcast(FP8X4),
                scales=scales[:, first:last],
                in_=grouped[u][:, tiles[0] : tiles[-1] + 1, :].rearrange("p i c -> p (i c)"),
            )
            nc.vector.reciprocal(
                out=inv_sum[u][:, tiles[0] : tiles[-1] + 1], in_=row_sum[u][:, tiles[0] : tiles[-1] + 1]
            )

        def weighted_sums(u, tiles=(0, 1)):
            b, t0 = u // PAIRS_PER_BATCH, 2 * (u % PAIRS_PER_BATCH)
            codes, scales = packed[u]
            if 0 in tiles:
                results[u] = packs.tile([P, 2, H], F32, tag="result", name="result")
            result = results[u]
            sums = {}
            for i in tiles:
                bank = sum_banks.tile([P, BANK], F32, tag="bank")
                for g in range(GROUPS):
                    cols = slice(P * (GROUPS * i + g), P * (GROUPS * i + g + 1))
                    nc.tensor.matmul_mx(
                        out=bank[:],
                        lhsT=codes[:, cols].bitcast(FP8X4),
                        lhsT_scale=scales[:, cols],
                        rhs=v_codes[b][:, g, :].bitcast(FP8X4),
                        rhs_scale=v_scales[b][:, g, :],
                        start=(g == 0),
                        stop=(g == GROUPS - 1),
                    )
                sums[i] = bank
            for i in tiles:
                if i == 0:
                    nc.vector.tensor_scalar(
                        out=result[:, i, :],
                        in0=sums[i][:],
                        scalar1=inv_sum[u][:, i : i + 1],
                        scalar2=None,
                        op0=ALU.mult,
                    )
                else:
                    nc.scalar.activation(
                        out=result[:, i, :],
                        in_=sums[i][:],
                        func=ACT.Copy,
                        scale=inv_sum[u][:, i : i + 1],
                    )
            nc.sync.dma_start(
                out=out_view[b][:, t0 + tiles[0] : t0 + tiles[-1] + 1, :],
                in_=result[:, tiles[0] : tiles[-1] + 1, :],
            )

        def load_values(n):
            b, g = n // GROUPS, n % GROUPS
            for u in range(2):
                value_rows[(n, u)] = packs.tile([P, 2, DIN], BF16, tag="result", name="value_rows")
                nc.sync.dma_start(
                    out=value_rows[(n, u)][:].rearrange("p i d -> p (i d)"), in_=v_view[b][g][:, u, :]
                )

        def queue_values(n, u):
            if u == 0:
                value_lined[n] = []
                for d in range(GROUPS):
                    value_lined[n].append(
                        packs.tile([P, 4 * BANK], BF16, tag="grouped", name="lined", align_bytes=64)
                    )
            words = value_rows[(n, u)][:].bitcast(F32)
            for d in range(GROUPS):
                queue_bank(
                    ("v", n, u, d),
                    [
                        words[:, i, PASS_WORDS * d + e : PASS_WORDS * (d + 1) : 2]
                        for i in range(2)
                        for e in range(2)
                    ],
                    keep_values,
                    (n, u, d),
                )

        def keep_values(n, u, d):
            nc.scalar.copy(
                out=value_lined[n][d][:].bitcast(F32)[:, BANK * u : BANK * (u + 1)].rearrange(
                    "p (i c e) -> p i c e", i=2, e=2
                ),
                in_=open_banks[("v", n, u, d)][:].rearrange("p (i e c) -> p i c e", i=2, e=2),
            )

        def quantise_values_in(n):
            codes = packs.tile([P, GROUPS, BANK], U32, tag="v_in_codes", bufs=1, align_bytes=64)
            scales = packs.tile([P, GROUPS, BANK], U8, tag="v_in_scales", bufs=1, align_bytes=64)
            for d in range(GROUPS):
                nc.vector.quantize_mx(
                    out=codes[:, d, :].bitcast(FP8X4), scales=scales[:, d, :], in_=value_lined[n][d][:]
                )
            value_in[n] = (codes, scales)

        def project_values(n):
            b, g = n // GROUPS, n % GROUPS
            codes, scales = value_in[n]
            lined = packs.tile([P, 4 * H], BF16, tag="v_grouped", bufs=1, align_bytes=64)
            for hb in range(H // P):
                h_cols = slice(P * hb, P * (hb + 1))
                bank = sum_banks.tile([P, BANK], F32, tag="bank")
                for t in range(PER_BANK):
                    t_cols = slice(P * t, P * (t + 1))
                    for d in range(GROUPS):
                        nc.tensor.matmul_mx(
                            out=bank[:, t_cols],
                            lhsT=codes[:, d, t_cols].bitcast(FP8X4),
                            lhsT_scale=scales[:, d, t_cols],
                            rhs=w_codes[:, d, h_cols].bitcast(FP8X4),
                            rhs_scale=w_scales[:, d, h_cols],
                            start=(d == 0),
                            stop=(d == GROUPS - 1),
                        )
                nc.vector.tensor_tensor(
                    out=lined[:, 4 * P * hb : 4 * P * (hb + 1)].rearrange("p (h t) -> p h t", t=4),
                    in0=bank[:].rearrange("p (t h) -> p h t", t=4),
                    in1=bias_rows[:, h_cols].unsqueeze(2).to_broadcast([P, P, 4]),
                    op=ALU.add,
                )
            nc.vector.quantize_mx(
                out=v_codes[b][:, g, :].bitcast(FP8X4), scales=v_scales[b][:, g, :], in_=lined[:]
            )

        def attend_front(x):
            if 0 <= x - 2 < PAIRS:
                quantise_weights(x - 2)
            if 0 <= x - 1 < PAIRS:
                queue_weights(x - 1, 0)
                queue_weights(x - 1, 1)
            if x < PAIRS:
                exponentials(x)

        def attend_back(x):
            if 0 <= x - 2 < PAIRS:
                weighted_sums(x - 2)

        for u in range(PLANS_AHEAD):
            load_plan(u)
        load_keys(0, 0)
        load_queries(0)
        load_gain()
        load_keys(0, 1)
        load_queries(1)
        load_values(0)
        load_weight()
        for w in range(2):
            queue_keys(0, 0, w)
        for w in range(2):
            queue_queries(0, w)
        write_waiting(1)
        load_queries(2)
        for w in range(2):
            queue_keys(0, 1, w)
        write_waiting(1)
        load_keys(1, 0)
        load_keys(1, 1)

        def queue_beside(r, i):
            if r < 2 * HALVES and r % 2 == 0:
                queue_values(r // 2, i)
            if r % 2 == 1 and (r + 1) // 2 < CHUNKS:
                queue_queries((r + 1) // 2, i)
            if KEYS_AT <= r < KEYS_AT + 2:
                queue_keys(1, r - KEYS_AT, i)

        x = 0
        logged = 0
        for r in range(PAIRS):
            for u in range(logged, min(PAIRS, logged + LOGS_PER_ROUND)):
                log_prior(u)
                if u == PAIRS - 1:
                    nc.scalar.activation(
                        out=exp_scale[:],
                        in_=z[u][:, 1, LK - 1 : LK],
                        func=ACT.Copy,
                        scale=0.0,
                        bias=INV_SQRT_H,
                    )
            logged = min(PAIRS, logged + LOGS_PER_ROUND)
            attends = 0 if r < FIRST_ATTEND else min(MOST_ATTENDS, r - x)
            if attends > 0:
                attend_front(x)
            queue_beside(r, 0)
            scores(r, 0)
            if attends > 0:
                attend_back(x)
                x += 1
            if r in BY_TILE:
                exponentials(r, (0,))
            if attends > 1:
                attend_front(x)
            queue_beside(r, 1)
            scores(r, 1)
            if r in BY_TILE:
                exponentials(r, (1,))
            if attends > 1:
                attend_back(x)
                x += 1
            if r < 2 * HALVES:
                n = r // 2
                if r % 2 == 0:
                    quantise_values_in(n)
                    if n + 1 < HALVES:
                        load_values(n + 1)
                else:
                    project_values(n)
            if r % 2 == 1 and (r + 1) // 2 + 2 < CHUNKS:
                load_queries((r + 1) // 2 + 2)
        last = PAIRS - 1
        quantise_weights(last - 2)
        for u in (last - 1, last):
            for i in range(2):
                queue_weights(u, i)
            if u == last - 1:
                write_waiting(1)
                weighted_sums(last - 2)
        write_waiting(1)
        quantise_weights(last - 1)
        weighted_sums(last - 1)
        for i in range(2):
            quantise_weights(last, (i,))
            weighted_sums(last, (i,))
